import numpy as np
import ml_dtypes


def mxq(x, axis, fmt="e4m3"):
    dtype, down = {"e4m3": (ml_dtypes.float8_e4m3fn, 7), "e5m2": (ml_dtypes.float8_e5m2, 14)}[fmt]
    v = np.moveaxis(np.asarray(x, np.float32).astype(ml_dtypes.bfloat16).astype(np.float64), axis, -1)
    blocks = v.reshape(v.shape[:-1] + (-1, 32))
    amax = np.abs(blocks).max(-1, keepdims=True)
    byte = np.maximum(np.where(amax > 0, np.frexp(amax)[1] - 1 + 127, 0) - down, 1)
    scale = np.exp2(byte - 127.0)
    codes = (blocks / scale).astype(np.float32).astype(dtype).astype(np.float64)
    return np.moveaxis((codes * scale).reshape(v.shape), -1, axis)


WIDE = False


def mx_kscale(k):
    if not WIDE:
        return np.ones(k)
    levels = np.array([10, -10, 5, -5, 0])
    a = np.random.permutation(np.resize(levels, k // 512 * 4)).reshape(k // 512, 4)
    idx = np.arange(k)
    return np.exp2(a[idx // 512, idx % 128 // 32])


BF16 = ml_dtypes.bfloat16


def bf(x):
    return np.asarray(x, np.float32).astype(BF16)


def f64(x):
    return np.asarray(x).astype(np.float64)


B, H0, W0, H1, W1, C = 8, 32, 48, 8, 16, 512
L, S = H0 * W0, H1 * W1
THR = 0.2
TEMPERATURE = 0.1
BORDER = 2
NM = min(L, S) // 2
ND = NM // 16
DUP = 0.92
RB = 0.5
ZT = 4.5
SD = ZT - np.sqrt(ZT**2 - 2.0 * np.log(min(L, S) * THR / (1.0 - THR)))
SIG = SD / np.sqrt(1.0 + RB**2 / 2.0)
G = np.sqrt(SIG * TEMPERATURE * np.sqrt(C / 2.0))
MATCH = np.log(max(L, S)) + SD**2 / 2.0 + 3.5
ALPHA = MATCH / (SIG * np.sqrt(C / 2.0))


def interior_mask(h, w, b):
    vh = (np.arange(h) >= b) & (np.arange(h) < h - b)
    vw = (np.arange(w) >= b) & (np.arange(w) < w - b)
    return (vh[:, None] & vw[None, :]).reshape(-1)


def softmax(v, axis):
    e = np.exp(v - v.max(axis=axis, keepdims=True))
    return e / e.sum(axis=axis, keepdims=True)


def pick(h, w):
    rep = np.random.permutation(np.flatnonzero(interior_mask(h, w, BORDER)))[:ND]
    rest = np.random.permutation(np.setdiff1d(np.arange(h * w), rep))[:NM]
    return rep, rest


def setup_inputs():
    s = mx_kscale(C)
    x0 = np.random.standard_normal((B, L, C))
    x1 = np.random.standard_normal((B, S, C))
    for n in range(B):
        r0, m0 = pick(H0, W0)
        r1, m1 = pick(H1, W1)
        x1[n, m1] = ALPHA * x0[n, m0] + np.sqrt(1.0 - ALPHA**2) * x1[n, m1]
        x0[n, r0] = DUP * x0[n, m0[:ND]]
        x1[n, r1] = DUP * x1[n, m1[:ND]]
    return {"feat_c0": bf(x0 * s),
            "feat_c1": bf(x1 * s),
            "W": bf(np.random.standard_normal((C, C)) * G / np.sqrt(C) / s[None, :]),
            "b": bf(np.random.standard_normal(C) * RB * G),
            "h0c": H0, "w0c": W0, "h1c": H1, "w1c": W1}


def reference(feat_c0, feat_c1, W, b, h0c, w0c, h1c, w1c):
    scale = feat_c0.shape[-1] ** 0.5
    wq = mxq(f64(W), 1, "e4m3")
    f0 = ((mxq(f64(feat_c0), 2, "e4m3") @ wq.T) + f64(b)) / scale
    f1 = ((mxq(f64(feat_c1), 2, "e4m3") @ wq.T) + f64(b)) / scale
    sim = (mxq(f0, 2, "e4m3") @ mxq(f1, 2, "e4m3").transpose(0, 2, 1)) / TEMPERATURE

    conf_0to1 = softmax(sim, 2)
    conf_1to0 = softmax(sim, 1)

    mask = (conf_0to1 > THR) & (conf_0to1 == conf_0to1.max(axis=2, keepdims=True))
    mask = mask | ((conf_1to0 > THR) & (conf_1to0 == conf_1to0.max(axis=1, keepdims=True)))

    mask = mask & interior_mask(h0c, w0c, BORDER)[None, :, None]
    mask = mask & interior_mask(h1c, w1c, BORDER)[None, None, :]

    mconf = np.where(mask, np.maximum(conf_0to1, conf_1to0), 0.0)
    return np.stack([conf_0to1, conf_1to0, mconf])

@@ -1,0 +1,361 @@
+from contextlib import ExitStack
+
+import concourse.mybir as mybir
+from concourse.masks import make_identity
+
+F32 = mybir.dt.float32
+BF16 = mybir.dt.bfloat16
+U32 = mybir.dt.uint32
+U8 = mybir.dt.uint8
+I32 = mybir.dt.int32
+FP8X4 = mybir.dt.float8_e4m3fn_x4
+ALU = mybir.AluOpType
+ACT = mybir.ActivationFunctionType
+AXIS = mybir.AxisListType
+
+P = 128
+PACK = 4
+FEAT = P * PACK
+TILES = 4
+CHUNK = TILES * P
+
+THR = 0.2
+TEMPERATURE = 0.1
+BORDER = 2
+FAR = 1.0e30
+
+FLOPS = 2 * (8 * 1536 + 8 * 128) * 512 * 512 + 2 * 8 * 1536 * 128 * 512
+
+
+def tile_coarsematching_t_kernel(tc, feat_c0, feat_c1, W, b, h0c, w0c, h1c, w1c, out):
+    nc = tc.nc
+    batches, cells0, feat = feat_c0.shape
+    cells1 = feat_c1.shape[1]
+    per_part = cells0 // P
+    banks = per_part // TILES
+    parts_per_row = w0c // per_part
+    assert feat == FEAT and cells1 == P and cells0 == h0c * w0c and cells1 == h1c * w1c
+    assert per_part % TILES == 0 and batches % TILES == 0 and parts_per_row == 4
+    in_rows = h1c - 2 * BORDER
+    in_cols = w1c - 2 * BORDER
+    shape = [P, per_part, in_rows, in_cols]
+
+    with ExitStack() as ctx:
+        keep = ctx.enter_context(tc.tile_pool(name="keep", bufs=1))
+        rows_pool = ctx.enter_context(tc.tile_pool(name="rows", bufs=3))
+        stage = ctx.enter_context(tc.tile_pool(name="stage", bufs=3))
+        codes_pool = ctx.enter_context(tc.tile_pool(name="codes", bufs=2))
+        planes = ctx.enter_context(tc.tile_pool(name="planes", bufs=2))
+        small = ctx.enter_context(tc.tile_pool(name="small", bufs=3))
+        psum_flip = ctx.enter_context(tc.psum_pool(name="psum_flip", bufs=2))
+        psum_proj = ctx.enter_context(tc.psum_pool(name="psum_proj", bufs=2))
+        psum_match = ctx.enter_context(tc.psum_pool(name="psum_match", bufs=4))
+
+        ident = keep.tile([P, P], F32)
+        make_identity(nc, ident[:])
+
+        part_i = keep.tile([P, per_part], I32)
+        nc.gpsimd.iota(part_i[:], pattern=[[0, per_part]], base=0, channel_multiplier=1)
+        j_i = keep.tile([P, per_part], I32)
+        nc.gpsimd.iota(j_i[:], pattern=[[1, per_part]], base=0, channel_multiplier=0)
+        sub_i = keep.tile([P, per_part], I32)
+        nc.vector.tensor_single_scalar(out=sub_i[:], in_=part_i[:], scalar=parts_per_row - 1, op=ALU.bitwise_and)
+        col = keep.tile([P, per_part], F32)
+        nc.vector.scalar_tensor_tensor(
+            out=col[:], in0=sub_i[:], scalar=float(per_part), in1=j_i[:], op0=ALU.mult, op1=ALU.add
+        )
+        inside = keep.tile([P, per_part], F32)
+        nc.vector.tensor_single_scalar(out=inside[:], in_=col[:], scalar=float(BORDER), op=ALU.is_ge)
+        nc.vector.scalar_tensor_tensor(
+            out=inside[:], in0=col[:], scalar=float(w0c - BORDER), in1=inside[:], op0=ALU.is_lt, op1=ALU.mult
+        )
+        nc.vector.scalar_tensor_tensor(
+            out=inside[:], in0=part_i[:], scalar=float(parts_per_row * BORDER), in1=inside[:],
+            op0=ALU.is_ge, op1=ALU.mult,
+        )
+        nc.vector.scalar_tensor_tensor(
+            out=inside[:], in0=part_i[:], scalar=float(parts_per_row * (h0c - BORDER)), in1=inside[:],
+            op0=ALU.is_lt, op1=ALU.mult,
+        )
+
+        mconf_tiles = []
+        for i in range(2):
+            mconf_tile = keep.tile([P, per_part, P], F32, name="mconf%d" % i)
+            nc.vector.memset(mconf_tile[:], 0.0)
+            mconf_tiles.append(mconf_tile)
+
+        def interior(plane):
+            grid = plane.rearrange("p j (r c) -> p j r c", c=w1c)
+            return grid[:, :, BORDER : h1c - BORDER, BORDER : w1c - BORDER]
+
+        f1_chunks = batches // TILES
+        n_chunks = f1_chunks + batches * banks
+        chunk_bytes = TILES * FEAT
+        f0_rows, f0_codes, f0_scales = {}, {}, {}
+        x_grouped, x_codes, x_scales, f_grouped = {}, {}, {}, {}
+
+        def flip_rows(rows):
+            words = rows.bitcast(F32)
+            grouped = stage.tile([P, CHUNK * PACK], BF16, tag="x_grouped", align_bytes=64)
+            grouped_words = grouped[:].bitcast(F32).rearrange("q (a r u) -> q a r u", a=TILES, u=2)
+            for pair in range(TILES // 2):
+                flipped = psum_flip.tile([P, 2, 2, P], F32, tag="flipped")
+                for a in range(2):
+                    for u in range(2):
+                        first = ((2 * pair + a) * 2 + u) * P
+                        nc.tensor.transpose(flipped[:, a, u, :], words[:, first : first + P], ident[:])
+                nc.scalar.copy(
+                    out=grouped_words[:, 2 * pair : 2 * pair + 2],
+                    in_=flipped[:].rearrange("q a u r -> q a r u"),
+                )
+            return grouped
+
+        def load_batch(n):
+            f0_rows[n] = rows_pool.tile([P, per_part * FEAT], BF16, tag="rows", name="f0_rows")
+            nc.sync.dma_start(out=f0_rows[n][:], in_=feat_c0[n].rearrange("(p j) k -> p (j k)", j=per_part))
+
+        def flip(i):
+            if i < f1_chunks:
+                rows = f1_rows[:, i * chunk_bytes : (i + 1) * chunk_bytes]
+            else:
+                n, c = divmod(i - f1_chunks, banks)
+                rows = f0_rows[n][:, c * chunk_bytes : (c + 1) * chunk_bytes]
+            x_grouped[i] = flip_rows(rows)
+
+        def quantise_x(i):
+            x_codes[i] = stage.tile([P, CHUNK], U32, tag="x_codes", name="x_codes", align_bytes=64)
+            x_scales[i] = stage.tile([P, CHUNK], U8, tag="x_scales", name="x_scales", align_bytes=64)
+            nc.vector.quantize_mx(out=x_codes[i][:].bitcast(FP8X4), scales=x_scales[i][:], in_=x_grouped[i][:])
+
+        def project(i):
+            f_grouped[i] = stage.tile([P, TILES, P, PACK], BF16, tag="f_grouped", name="f_grouped", align_bytes=64)
+            for a in range(TILES):
+                acc = psum_proj.tile([P, PACK, P], F32, tag="acc")
+                x_cols = slice(a * P, (a + 1) * P)
+                for t in range(PACK):
+                    w_cols = slice(t * P, (t + 1) * P)
+                    nc.tensor.matmul_mx(
+                        out=acc[:, t, :],
+                        lhsT=w_codes[:, w_cols].bitcast(FP8X4),
+                        lhsT_scale=w_scales[:, w_cols],
+                        rhs=x_codes[i][:, x_cols].bitcast(FP8X4),
+                        rhs_scale=x_scales[i][:, x_cols],
+                        start=True,
+                        stop=True,
+                    )
+                nc.vector.scalar_tensor_tensor(
+                    out=f_grouped[i][:, a],
+                    in0=acc[:].rearrange("p t r -> p r t"),
+                    scalar=inv_scale,
+                    in1=bias_by_row,
+                    op0=ALU.mult,
+                    op1=ALU.add,
+                )
+
+        def quantise_f(i):
+            if i < f1_chunks:
+                codes, scales, c = f1_codes, f1_scales, i
+            else:
+                n, c = divmod(i - f1_chunks, banks)
+                if c == 0:
+                    f0_codes[n] = codes_pool.tile([P, cells0], U32, tag="f0_codes", name="f0_codes", align_bytes=64)
+                    f0_scales[n] = codes_pool.tile([P, cells0], U8, tag="f0_scales", name="f0_scales", align_bytes=64)
+                codes, scales = f0_codes[n], f0_scales[n]
+            cols = slice(c * CHUNK, (c + 1) * CHUNK)
+            nc.vector.quantize_mx(
+                out=codes[:, cols].bitcast(FP8X4),
+                scales=scales[:, cols],
+                in_=f_grouped[i][:].rearrange("p a r t -> p (a r t)"),
+            )
+
+        w_rows = keep.tile([P, PACK * FEAT], BF16)
+        nc.sync.dma_start(out=w_rows[:], in_=W.rearrange("(p t) k -> p (t k)", t=PACK))
+        f1_rows = keep.tile([P, batches * FEAT], BF16)
+        nc.sync.dma_start(
+            out=f1_rows[:].rearrange("s (n k) -> s n k", n=batches), in_=feat_c1.rearrange("n s k -> s n k")
+        )
+        b_raw = keep.tile([P, PACK], BF16)
+        nc.sync.dma_start(out=b_raw[:], in_=b.rearrange("(p t) -> p t", t=PACK))
+        load_batch(0)
+        load_batch(1)
+
+        w_codes = keep.tile([P, FEAT], U32, align_bytes=64)
+        w_scales = keep.tile([P, FEAT], U8, align_bytes=64)
+        w_grouped = flip_rows(w_rows[:])
+        nc.vector.quantize_mx(out=w_codes[:].bitcast(FP8X4), scales=w_scales[:], in_=w_grouped[:])
+        f1_codes = keep.tile([P, batches * P], U32, align_bytes=64)
+        f1_scales = keep.tile([P, batches * P], U8, align_bytes=64)
+
+        inv_scale = 1.0 / float(FEAT) ** 0.5
+        bias = keep.tile([P, PACK], F32)
+        nc.vector.tensor_single_scalar(out=bias[:], in_=b_raw[:], scalar=inv_scale, op=ALU.mult)
+        bias_by_row = bias[:].unsqueeze(1).to_broadcast([P, P, PACK])
+
+        live = {}
+        inv_temp = 1.0 / TEMPERATURE
+
+        def by_cell(per_cell):
+            return per_cell.unsqueeze(2).unsqueeze(3).to_broadcast(shape)
+
+        def out_plane(k, n):
+            return out[k, n].rearrange("(p j) s -> p j s", j=per_part)
+
+        def phase_rows(n):
+            n_cols = slice(n * P, (n + 1) * P)
+            row_max = small.tile([P, per_part], F32, tag="row_max")
+            shift0 = small.tile([P, per_part], F32, tag="shift0")
+            row_sum = small.tile([P, per_part], F32, tag="row_sum")
+            col_max_bank = small.tile([P, banks, P], F32, tag="col_max_bank")
+            conf0 = planes.tile([P, per_part, P], F32, tag="conf0")
+            sim_in = planes.tile(shape, F32, tag="sim_in")
+            for c in range(banks):
+                sim = psum_match.tile([P, TILES, P], F32, tag="match")
+                for a in range(TILES):
+                    j_cols = slice((c * TILES + a) * P, (c * TILES + a + 1) * P)
+                    nc.tensor.matmul_mx(
+                        out=sim[:, a, :],
+                        lhsT=f0_codes[n][:, j_cols].bitcast(FP8X4),
+                        lhsT_scale=f0_scales[n][:, j_cols],
+                        rhs=f1_codes[:, n_cols].bitcast(FP8X4),
+                        rhs_scale=f1_scales[:, n_cols],
+                        start=True,
+                        stop=True,
+                    )
+                js = slice(c * TILES, (c + 1) * TILES)
+                nc.vector.tensor_reduce(out=row_max[:, js], in_=sim[:], axis=AXIS.X, op=ALU.max)
+                nc.vector.tensor_reduce(
+                    out=col_max_bank[:, c, :], in_=sim[:].rearrange("p a s -> p s a"), axis=AXIS.X, op=ALU.max
+                )
+                nc.vector.tensor_single_scalar(out=shift0[:, js], in_=row_max[:, js], scalar=-inv_temp, op=ALU.mult)
+                for a in range(TILES):
+                    j = c * TILES + a
+                    nc.scalar.activation(
+                        out=conf0[:, j, :],
+                        in_=sim[:, a, :],
+                        func=ACT.Exp,
+                        bias=shift0[:, j : j + 1],
+                        scale=inv_temp,
+                        accum_out=row_sum[:, j : j + 1],
+                    )
+                nc.scalar.copy(out=sim_in[:, js], in_=interior(sim[:]))
+            col_max_part = small.tile([P, P], F32, tag="col_max_part")
+            nc.vector.tensor_reduce(
+                out=col_max_part[:], in_=col_max_bank[:].rearrange("p c s -> p s c"), axis=AXIS.X, op=ALU.max
+            )
+            col_max_t = psum_match.tile([P, P], F32, tag="match")
+            nc.tensor.transpose(col_max_t[:], col_max_part[:], ident[:])
+            live["row_max", n], live["row_sum", n], live["col_max_t", n] = row_max, row_sum, col_max_t
+            live["conf0", n], live["sim_in", n] = conf0, sim_in
+
+        def phase_columns(n):
+            n_cols = slice(n * P, (n + 1) * P)
+            conf0 = live["conf0", n]
+            col_max = small.tile([P, 1], F32, tag="col_max")
+            nc.vector.tensor_reduce(out=col_max[:], in_=live["col_max_t", n][:], axis=AXIS.X, op=ALU.max)
+            shift1 = small.tile([P, 1], F32, tag="shift1")
+            nc.vector.tensor_single_scalar(out=shift1[:], in_=col_max[:], scalar=-inv_temp, op=ALU.mult)
+            recip0 = small.tile([P, per_part], F32, tag="recip0")
+            nc.vector.reciprocal(out=recip0[:], in_=live["row_sum", n][:])
+            conf1_t = planes.tile([P, cells0], F32, tag="conf1_t")
+            col_sum = small.tile([P, banks], F32, tag="col_sum")
+            for c in range(banks):
+                cols = slice(c * CHUNK, (c + 1) * CHUNK)
+                sim_t = psum_match.tile([P, CHUNK], F32, tag="match")
+                nc.tensor.matmul_mx(
+                    out=sim_t[:],
+                    lhsT=f1_codes[:, n_cols].bitcast(FP8X4),
+                    lhsT_scale=f1_scales[:, n_cols],
+                    rhs=f0_codes[n][:, cols].bitcast(FP8X4),
+                    rhs_scale=f0_scales[n][:, cols],
+                    start=True,
+                    stop=True,
+                )
+                nc.scalar.activation(
+                    out=conf1_t[:, cols],
+                    in_=sim_t[:],
+                    func=ACT.Exp,
+                    bias=shift1[:],
+                    scale=inv_temp,
+                    accum_out=col_sum[:, c : c + 1],
+                )
+            for j in range(per_part):
+                nc.scalar.activation(out=conf0[:, j, :], in_=conf0[:, j, :], func=ACT.Copy, scale=recip0[:, j : j + 1])
+            nc.sync.dma_start(out=out_plane(0, n), in_=conf0[:])
+            goal0 = small.tile([P, per_part], F32, tag="goal0")
+            nc.gpsimd.tensor_scalar(out=goal0[:], in0=recip0[:], scalar1=THR, scalar2=FAR, op0=ALU.is_le, op1=ALU.mult)
+            nc.gpsimd.tensor_tensor(out=goal0[:], in0=goal0[:], in1=live["row_max", n][:], op=ALU.add)
+            miss = planes.tile(shape, F32, tag="miss")
+            nc.gpsimd.tensor_tensor(out=miss[:], in0=live["sim_in", n][:], in1=by_cell(goal0[:]), op=ALU.subtract)
+            nc.scalar.activation(out=miss[:], in_=miss[:], func=ACT.Sign)
+            live["col_max", n], live["col_sum", n], live["conf1_t", n], live["miss", n] = col_max, col_sum, conf1_t, miss
+
+        def phase_back(n):
+            conf1_t, miss = live["conf1_t", n], live["miss", n]
+            recip1 = small.tile([P, 1], F32, tag="recip1")
+            nc.vector.tensor_reduce(out=recip1[:], in_=live["col_sum", n][:], axis=AXIS.X, op=ALU.add)
+            nc.vector.reciprocal(out=recip1[:], in_=recip1[:])
+            nc.gpsimd.tensor_scalar(
+                out=conf1_t[:], in0=conf1_t[:], scalar1=recip1[:], scalar2=1.0, op0=ALU.mult, op1=ALU.mult
+            )
+            goal1 = small.tile([P, 1], F32, tag="goal1")
+            nc.vector.tensor_scalar(out=goal1[:], in0=recip1[:], scalar1=THR, scalar2=FAR, op0=ALU.is_le, op1=ALU.mult)
+            nc.vector.tensor_tensor(out=goal1[:], in0=goal1[:], in1=live["col_max", n][:], op=ALU.add)
+            goal1_rep = small.tile([P, P], F32, tag="goal1_rep")
+            nc.vector.tensor_copy(out=goal1_rep[:], in_=goal1[:].to_broadcast([P, P]))
+            goal1_bank = psum_match.tile([P, P], F32, tag="match")
+            nc.tensor.transpose(goal1_bank[:], goal1_rep[:], ident[:])
+            goal1_all = small.tile([P, 1, P], F32, tag="goal1_all")
+            nc.scalar.copy(out=goal1_all[:, 0, :], in_=goal1_bank[:])
+            conf1 = planes.tile([P, per_part, P], F32, tag="conf1")
+            for c in range(banks):
+                conf1_bank = psum_match.tile([P, TILES, P], F32, tag="match")
+                for a in range(TILES):
+                    j = c * TILES + a
+                    nc.tensor.transpose(conf1_bank[:, a, :], conf1_t[:, j * P : (j + 1) * P], ident[:])
+                nc.scalar.copy(out=conf1[:, c * TILES : (c + 1) * TILES, :], in_=conf1_bank[:])
+            nc.sync.dma_start(out=out_plane(1, n), in_=conf1[:])
+            gap1 = planes.tile(shape, F32, tag="gap1")
+            nc.gpsimd.tensor_tensor(
+                out=gap1[:], in0=live["sim_in", n][:], in1=interior(goal1_all[:]).to_broadcast(shape), op=ALU.subtract
+            )
+            nc.gpsimd.tensor_tensor(out=miss[:], in0=miss[:], in1=gap1[:], op=ALU.mult)
+            live["conf1", n] = conf1
+
+        def phase_mconf(n):
+            larger = planes.tile(shape, F32, tag="larger")
+            nc.vector.tensor_tensor(
+                out=larger[:], in0=interior(live["conf0", n][:]), in1=interior(live["conf1", n][:]), op=ALU.max
+            )
+            nc.vector.scalar_tensor_tensor(
+                out=larger[:].rearrange("p j r c -> p (j r c)"),
+                in0=live["miss", n][:].rearrange("p j r c -> p (j r c)"),
+                scalar=0.0,
+                in1=larger[:].rearrange("p j r c -> p (j r c)"),
+                op0=ALU.is_equal,
+                op1=ALU.mult,
+            )
+            mconf = mconf_tiles[n % 2]
+            nc.gpsimd.tensor_tensor(out=interior(mconf[:]), in0=larger[:], in1=by_cell(inside[:]), op=ALU.mult)
+            nc.sync.dma_start(out=out_plane(2, n), in_=mconf[:])
+
+        phases = [phase_rows, phase_columns, phase_back, phase_mconf]
+        first_phase = f1_chunks + banks
+        flip(0)
+        flip(1)
+        quantise_x(0)
+        for i in range(n_chunks + len(phases)):
+            n, c = divmod(i, banks)
+            if c == 0 and n + 2 < batches:
+                load_batch(n + 2)
+            if 1 <= i <= n_chunks:
+                quantise_f(i - 1)
+            if i < n_chunks:
+                project(i)
+            if i + 2 < n_chunks:
+                flip(i + 2)
+            if i + 1 < n_chunks:
+                quantise_x(i + 1)
+            for k in reversed(range(len(phases))):
+                n, c = divmod(i - first_phase - k, banks)
+                if c == 0 and 0 <= n < batches:
+                    phases[k](n)

@@ -226,7 +226,7 @@ def tile_coarsematching_t_kernel(tc, feat_c0, feat_c1, W, b, h0c, w0c, h1c, w1c,
                 nc.vector.tensor_reduce(
                     out=col_max_bank[:, c, :], in_=sim[:].rearrange("p a s -> p s a"), axis=AXIS.X, op=ALU.max
                 )
-                nc.vector.tensor_single_scalar(out=shift0[:, js], in_=row_max[:, js], scalar=-inv_temp, op=ALU.mult)
+                nc.scalar.mul(out=shift0[:, js], in_=row_max[:, js], mul=-inv_temp)
                 for a in range(TILES):
                     j = c * TILES + a
                     nc.scalar.activation(
@@ -253,7 +253,7 @@ def tile_coarsematching_t_kernel(tc, feat_c0, feat_c1, W, b, h0c, w0c, h1c, w1c,
             col_max = small.tile([P, 1], F32, tag="col_max")
             nc.vector.tensor_reduce(out=col_max[:], in_=live["col_max_t", n][:], axis=AXIS.X, op=ALU.max)
             shift1 = small.tile([P, 1], F32, tag="shift1")
-            nc.vector.tensor_single_scalar(out=shift1[:], in_=col_max[:], scalar=-inv_temp, op=ALU.mult)
+            nc.scalar.mul(out=shift1[:], in_=col_max[:], mul=-inv_temp)
             recip0 = small.tile([P, per_part], F32, tag="recip0")
             nc.vector.reciprocal(out=recip0[:], in_=live["row_sum", n][:])
             conf1_t = planes.tile([P, cells0], F32, tag="conf1_t")
@@ -294,9 +294,8 @@ def tile_coarsematching_t_kernel(tc, feat_c0, feat_c1, W, b, h0c, w0c, h1c, w1c,
             recip1 = small.tile([P, 1], F32, tag="recip1")
             nc.vector.tensor_reduce(out=recip1[:], in_=live["col_sum", n][:], axis=AXIS.X, op=ALU.add)
             nc.vector.reciprocal(out=recip1[:], in_=recip1[:])
-            nc.gpsimd.tensor_scalar(
-                out=conf1_t[:], in0=conf1_t[:], scalar1=recip1[:], scalar2=1.0, op0=ALU.mult, op1=ALU.mult
-            )
+            recip1_diag = small.tile([P, P], F32, tag="recip1_diag")
+            nc.vector.tensor_scalar_mul(out=recip1_diag[:], in0=ident[:], scalar1=recip1[:])
             goal1 = small.tile([P, 1], F32, tag="goal1")
             nc.vector.tensor_scalar(out=goal1[:], in0=recip1[:], scalar1=THR, scalar2=FAR, op0=ALU.is_le, op1=ALU.mult)
             nc.vector.tensor_tensor(out=goal1[:], in0=goal1[:], in1=live["col_max", n][:], op=ALU.add)
@@ -311,7 +310,13 @@ def tile_coarsematching_t_kernel(tc, feat_c0, feat_c1, W, b, h0c, w0c, h1c, w1c,
                 conf1_bank = psum_match.tile([P, TILES, P], F32, tag="match")
                 for a in range(TILES):
                     j = c * TILES + a
-                    nc.tensor.transpose(conf1_bank[:, a, :], conf1_t[:, j * P : (j + 1) * P], ident[:])
+                    nc.tensor.matmul(
+                        out=conf1_bank[:, a, :],
+                        lhsT=conf1_t[:, j * P : (j + 1) * P],
+                        rhs=recip1_diag[:],
+                        start=True,
+                        stop=True,
+                    )
                 nc.scalar.copy(out=conf1[:, c * TILES : (c + 1) * TILES, :], in_=conf1_bank[:])
             nc.sync.dma_start(out=out_plane(1, n), in_=conf1[:])
             gap1 = planes.tile(shape, F32, tag="gap1")

@@ -22,6 +22,7 @@ CHUNK = TILES * P
 THR = 0.2
 TEMPERATURE = 0.1
 BORDER = 2
+PHASE_GAP = 2
 FAR = 1.0e30
 
 FLOPS = 2 * (8 * 1536 + 8 * 128) * 512 * 512 + 2 * 8 * 1536 * 128 * 512
@@ -45,11 +46,11 @@ def tile_coarsematching_t_kernel(tc, feat_c0, feat_c1, W, b, h0c, w0c, h1c, w1c,
         rows_pool = ctx.enter_context(tc.tile_pool(name="rows", bufs=3))
         stage = ctx.enter_context(tc.tile_pool(name="stage", bufs=3))
         codes_pool = ctx.enter_context(tc.tile_pool(name="codes", bufs=2))
-        planes = ctx.enter_context(tc.tile_pool(name="planes", bufs=2))
-        small = ctx.enter_context(tc.tile_pool(name="small", bufs=3))
+        planes = ctx.enter_context(tc.tile_pool(name="planes", bufs=3))
+        small = ctx.enter_context(tc.tile_pool(name="small", bufs=4))
         psum_flip = ctx.enter_context(tc.psum_pool(name="psum_flip", bufs=2))
-        psum_proj = ctx.enter_context(tc.psum_pool(name="psum_proj", bufs=2))
-        psum_match = ctx.enter_context(tc.psum_pool(name="psum_match", bufs=4))
+        psum_proj = ctx.enter_context(tc.psum_pool(name="psum_proj", bufs=3))
+        psum_match = ctx.enter_context(tc.psum_pool(name="psum_match", bufs=3))
 
         ident = keep.tile([P, P], F32)
         make_identity(nc, ident[:])
@@ -200,52 +201,57 @@ def tile_coarsematching_t_kernel(tc, feat_c0, feat_c1, W, b, h0c, w0c, h1c, w1c,
         def out_plane(k, n):
             return out[k, n].rearrange("(p j) s -> p j s", j=per_part)
 
-        def phase_rows(n):
+        def rows_chunk(n, c):
+            if c == 0:
+                live["row_max", n] = small.tile([P, per_part], F32, tag="row_max", name="row_max")
+                live["shift0", n] = small.tile([P, per_part], F32, tag="shift0", name="shift0")
+                live["row_sum", n] = small.tile([P, per_part], F32, tag="row_sum", name="row_sum")
+                live["col_max_bank", n] = small.tile([P, banks, P], F32, tag="col_max_bank", name="col_max_bank")
+                live["conf0", n] = planes.tile([P, per_part, P], F32, tag="conf0", name="conf0")
+                live["sim_in", n] = planes.tile(shape, F32, tag="sim_in", name="sim_in")
+            row_max, shift0, row_sum = live["row_max", n], live["shift0", n], live["row_sum", n]
             n_cols = slice(n * P, (n + 1) * P)
-            row_max = small.tile([P, per_part], F32, tag="row_max")
-            shift0 = small.tile([P, per_part], F32, tag="shift0")
-            row_sum = small.tile([P, per_part], F32, tag="row_sum")
-            col_max_bank = small.tile([P, banks, P], F32, tag="col_max_bank")
-            conf0 = planes.tile([P, per_part, P], F32, tag="conf0")
-            sim_in = planes.tile(shape, F32, tag="sim_in")
-            for c in range(banks):
-                sim = psum_match.tile([P, TILES, P], F32, tag="match")
-                for a in range(TILES):
-                    j_cols = slice((c * TILES + a) * P, (c * TILES + a + 1) * P)
-                    nc.tensor.matmul_mx(
-                        out=sim[:, a, :],
-                        lhsT=f0_codes[n][:, j_cols].bitcast(FP8X4),
-                        lhsT_scale=f0_scales[n][:, j_cols],
-                        rhs=f1_codes[:, n_cols].bitcast(FP8X4),
-                        rhs_scale=f1_scales[:, n_cols],
-                        start=True,
-                        stop=True,
-                    )
-                js = slice(c * TILES, (c + 1) * TILES)
-                nc.vector.tensor_reduce(out=row_max[:, js], in_=sim[:], axis=AXIS.X, op=ALU.max)
-                nc.vector.tensor_reduce(
-                    out=col_max_bank[:, c, :], in_=sim[:].rearrange("p a s -> p s a"), axis=AXIS.X, op=ALU.max
+            sim = psum_match.tile([P, TILES, P], F32, tag="match")
+            for a in range(TILES):
+                j_cols = slice((c * TILES + a) * P, (c * TILES + a + 1) * P)
+                nc.tensor.matmul_mx(
+                    out=sim[:, a, :],
+                    lhsT=f0_codes[n][:, j_cols].bitcast(FP8X4),
+                    lhsT_scale=f0_scales[n][:, j_cols],
+                    rhs=f1_codes[:, n_cols].bitcast(FP8X4),
+                    rhs_scale=f1_scales[:, n_cols],
+                    start=True,
+                    stop=True,
                 )
-                nc.scalar.mul(out=shift0[:, js], in_=row_max[:, js], mul=-inv_temp)
-                for a in range(TILES):
-                    j = c * TILES + a
-                    nc.scalar.activation(
-                        out=conf0[:, j, :],
-                        in_=sim[:, a, :],
-                        func=ACT.Exp,
-                        bias=shift0[:, j : j + 1],
-                        scale=inv_temp,
-                        accum_out=row_sum[:, j : j + 1],
-                    )
-                nc.scalar.copy(out=sim_in[:, js], in_=interior(sim[:]))
+            js = slice(c * TILES, (c + 1) * TILES)
+            nc.vector.tensor_reduce(out=row_max[:, js], in_=sim[:], axis=AXIS.X, op=ALU.max)
+            nc.vector.tensor_reduce(
+                out=live["col_max_bank", n][:, c, :], in_=sim[:].rearrange("p a s -> p s a"), axis=AXIS.X, op=ALU.max
+            )
+            nc.scalar.mul(out=shift0[:, js], in_=row_max[:, js], mul=-inv_temp)
+            for a in range(TILES):
+                j = c * TILES + a
+                nc.scalar.activation(
+                    out=live["conf0", n][:, j, :],
+                    in_=sim[:, a, :],
+                    func=ACT.Exp,
+                    bias=shift0[:, j : j + 1],
+                    scale=inv_temp,
+                    accum_out=row_sum[:, j : j + 1],
+                )
+            nc.scalar.copy(out=live["sim_in", n][:, js], in_=interior(sim[:]))
+
+        def column_maxima(n):
             col_max_part = small.tile([P, P], F32, tag="col_max_part")
             nc.vector.tensor_reduce(
-                out=col_max_part[:], in_=col_max_bank[:].rearrange("p c s -> p s c"), axis=AXIS.X, op=ALU.max
+                out=col_max_part[:],
+                in_=live["col_max_bank", n][:].rearrange("p c s -> p s c"),
+                axis=AXIS.X,
+                op=ALU.max,
             )
-            col_max_t = psum_match.tile([P, P], F32, tag="match")
+            col_max_t = psum_flip.tile([P, P], F32, tag="flipped")
             nc.tensor.transpose(col_max_t[:], col_max_part[:], ident[:])
-            live["row_max", n], live["row_sum", n], live["col_max_t", n] = row_max, row_sum, col_max_t
-            live["conf0", n], live["sim_in", n] = conf0, sim_in
+            live["col_max_t", n] = col_max_t
 
         def phase_columns(n):
             n_cols = slice(n * P, (n + 1) * P)
@@ -301,7 +307,7 @@ def tile_coarsematching_t_kernel(tc, feat_c0, feat_c1, W, b, h0c, w0c, h1c, w1c,
             nc.vector.tensor_tensor(out=goal1[:], in0=goal1[:], in1=live["col_max", n][:], op=ALU.add)
             goal1_rep = small.tile([P, P], F32, tag="goal1_rep")
             nc.vector.tensor_copy(out=goal1_rep[:], in_=goal1[:].to_broadcast([P, P]))
-            goal1_bank = psum_match.tile([P, P], F32, tag="match")
+            goal1_bank = psum_flip.tile([P, P], F32, tag="flipped")
             nc.tensor.transpose(goal1_bank[:], goal1_rep[:], ident[:])
             goal1_all = small.tile([P, 1, P], F32, tag="goal1_all")
             nc.scalar.copy(out=goal1_all[:, 0, :], in_=goal1_bank[:])
@@ -343,12 +349,11 @@ def tile_coarsematching_t_kernel(tc, feat_c0, feat_c1, W, b, h0c, w0c, h1c, w1c,
             nc.gpsimd.tensor_tensor(out=interior(mconf[:]), in0=larger[:], in1=by_cell(inside[:]), op=ALU.mult)
             nc.sync.dma_start(out=out_plane(2, n), in_=mconf[:])
 
-        phases = [phase_rows, phase_columns, phase_back, phase_mconf]
-        first_phase = f1_chunks + banks
+        phases = [phase_columns, phase_back, phase_mconf]
         flip(0)
         flip(1)
         quantise_x(0)
-        for i in range(n_chunks + len(phases)):
+        for i in range(n_chunks + 2 + PHASE_GAP * (len(phases) - 1)):
             n, c = divmod(i, banks)
             if c == 0 and n + 2 < batches:
                 load_batch(n + 2)
@@ -361,6 +366,11 @@ def tile_coarsematching_t_kernel(tc, feat_c0, feat_c1, W, b, h0c, w0c, h1c, w1c,
             if i + 1 < n_chunks:
                 quantise_x(i + 1)
             for k in reversed(range(len(phases))):
-                n, c = divmod(i - first_phase - k, banks)
-                if c == 0 and 0 <= n < batches:
+                n, c = divmod(i - 2 - PHASE_GAP * k - f1_chunks, banks)
+                if c == banks - 1 and 0 <= n < batches:
                     phases[k](n)
+            n, c = divmod(i - 1 - f1_chunks, banks)
+            if 0 <= n < batches:
+                rows_chunk(n, c)
+                if c == banks - 1:
+                    column_maxima(n)

@@ -22,8 +22,17 @@ CHUNK = TILES * P
 THR = 0.2
 TEMPERATURE = 0.1
 BORDER = 2
-PHASE_GAP = 2
 FAR = 1.0e30
+
+FLIP = -2
+QUANTISE_X = -1
+PROJECT = 0
+ROWS = 1
+FINISH_ROWS = 2
+COLUMNS = 4
+BACK = 7
+MCONF = 8
+LEAD = 2
 
 FLOPS = 2 * (8 * 1536 + 8 * 128) * 512 * 512 + 2 * 8 * 1536 * 128 * 512
 
@@ -36,21 +45,23 @@ def tile_coarsematching_t_kernel(tc, feat_c0, feat_c1, W, b, h0c, w0c, h1c, w1c,
     banks = per_part // TILES
     parts_per_row = w0c // per_part
     assert feat == FEAT and cells1 == P and cells0 == h0c * w0c and cells1 == h1c * w1c
-    assert per_part % TILES == 0 and batches % TILES == 0 and parts_per_row == 4
+    assert per_part % TILES == 0 and batches % TILES == 0 and parts_per_row == 4 and BORDER == 2
     in_rows = h1c - 2 * BORDER
     in_cols = w1c - 2 * BORDER
-    shape = [P, per_part, in_rows, in_cols]
+    shape = [P, TILES, in_rows, in_cols]
 
     with ExitStack() as ctx:
         keep = ctx.enter_context(tc.tile_pool(name="keep", bufs=1))
         rows_pool = ctx.enter_context(tc.tile_pool(name="rows", bufs=3))
         stage = ctx.enter_context(tc.tile_pool(name="stage", bufs=3))
-        codes_pool = ctx.enter_context(tc.tile_pool(name="codes", bufs=2))
-        planes = ctx.enter_context(tc.tile_pool(name="planes", bufs=3))
-        small = ctx.enter_context(tc.tile_pool(name="small", bufs=4))
+        to_columns = ctx.enter_context(tc.tile_pool(name="to_columns", bufs=COLUMNS - ROWS + 2))
+        to_back = ctx.enter_context(tc.tile_pool(name="to_back", bufs=BACK - COLUMNS + 2))
+        to_mconf = ctx.enter_context(tc.tile_pool(name="to_mconf", bufs=MCONF - ROWS + 2))
+        late = ctx.enter_context(tc.tile_pool(name="late", bufs=3))
+        by_batch = ctx.enter_context(tc.tile_pool(name="by_batch", bufs=(BACK - ROWS) // banks + 3))
         psum_flip = ctx.enter_context(tc.psum_pool(name="psum_flip", bufs=2))
-        psum_proj = ctx.enter_context(tc.psum_pool(name="psum_proj", bufs=3))
-        psum_match = ctx.enter_context(tc.psum_pool(name="psum_match", bufs=3))
+        psum_proj = ctx.enter_context(tc.psum_pool(name="psum_proj", bufs=LEAD + 1))
+        psum_match = ctx.enter_context(tc.psum_pool(name="psum_match", bufs=1))
 
         ident = keep.tile([P, P], F32)
         make_identity(nc, ident[:])
@@ -78,10 +89,12 @@ def tile_coarsematching_t_kernel(tc, feat_c0, feat_c1, W, b, h0c, w0c, h1c, w1c,
             out=inside[:], in0=part_i[:], scalar=float(parts_per_row * (h0c - BORDER)), in1=inside[:],
             op0=ALU.is_lt, op1=ALU.mult,
         )
+        sink = keep.tile([P, per_part], F32)
+        nc.vector.tensor_scalar(out=sink[:], in0=inside[:], scalar1=1.0, scalar2=FAR, op0=ALU.subtract, op1=ALU.mult)
 
         mconf_tiles = []
-        for i in range(2):
-            mconf_tile = keep.tile([P, per_part, P], F32, name="mconf%d" % i)
+        for c in range(2 * banks):
+            mconf_tile = keep.tile([P, TILES, P], F32, name="mconf%d" % c)
             nc.vector.memset(mconf_tile[:], 0.0)
             mconf_tiles.append(mconf_tile)
 
@@ -91,9 +104,19 @@ def tile_coarsematching_t_kernel(tc, feat_c0, feat_c1, W, b, h0c, w0c, h1c, w1c,
 
         f1_chunks = batches // TILES
         n_chunks = f1_chunks + batches * banks
-        chunk_bytes = TILES * FEAT
-        f0_rows, f0_codes, f0_scales = {}, {}, {}
-        x_grouped, x_codes, x_scales, f_grouped = {}, {}, {}, {}
+        chunk_elems = TILES * FEAT
+        f0_rows = {}
+        x_grouped, x_codes, x_scales, f_grouped, f0_codes, f0_scales = {}, {}, {}, {}, {}, {}
+        acc = {}
+
+        def is_chunk(i):
+            return 0 <= i < n_chunks
+
+        def is_f0_chunk(i):
+            return f1_chunks <= i < n_chunks
+
+        def batch_and_bank(i):
+            return divmod(i - f1_chunks, banks)
 
         def flip_rows(rows):
             words = rows.bitcast(F32)
@@ -117,10 +140,10 @@ def tile_coarsematching_t_kernel(tc, feat_c0, feat_c1, W, b, h0c, w0c, h1c, w1c,
 
         def flip(i):
             if i < f1_chunks:
-                rows = f1_rows[:, i * chunk_bytes : (i + 1) * chunk_bytes]
+                rows = f1_rows[:, i * chunk_elems : (i + 1) * chunk_elems]
             else:
-                n, c = divmod(i - f1_chunks, banks)
-                rows = f0_rows[n][:, c * chunk_bytes : (c + 1) * chunk_bytes]
+                n, c = batch_and_bank(i)
+                rows = f0_rows[n][:, c * chunk_elems : (c + 1) * chunk_elems]
             x_grouped[i] = flip_rows(rows)
 
         def quantise_x(i):
@@ -128,53 +151,244 @@ def tile_coarsematching_t_kernel(tc, feat_c0, feat_c1, W, b, h0c, w0c, h1c, w1c,
             x_scales[i] = stage.tile([P, CHUNK], U8, tag="x_scales", name="x_scales", align_bytes=64)
             nc.vector.quantize_mx(out=x_codes[i][:].bitcast(FP8X4), scales=x_scales[i][:], in_=x_grouped[i][:])
 
-        def project(i):
-            f_grouped[i] = stage.tile([P, TILES, P, PACK], BF16, tag="f_grouped", name="f_grouped", align_bytes=64)
-            for a in range(TILES):
-                acc = psum_proj.tile([P, PACK, P], F32, tag="acc")
-                x_cols = slice(a * P, (a + 1) * P)
-                for t in range(PACK):
-                    w_cols = slice(t * P, (t + 1) * P)
-                    nc.tensor.matmul_mx(
-                        out=acc[:, t, :],
-                        lhsT=w_codes[:, w_cols].bitcast(FP8X4),
-                        lhsT_scale=w_scales[:, w_cols],
-                        rhs=x_codes[i][:, x_cols].bitcast(FP8X4),
-                        rhs_scale=x_scales[i][:, x_cols],
-                        start=True,
-                        stop=True,
-                    )
-                nc.vector.scalar_tensor_tensor(
-                    out=f_grouped[i][:, a],
-                    in0=acc[:].rearrange("p t r -> p r t"),
-                    scalar=inv_scale,
-                    in1=bias_by_row,
-                    op0=ALU.mult,
-                    op1=ALU.add,
+        def project_tile(g):
+            i, a = divmod(g, TILES)
+            acc[g] = psum_proj.tile([P, PACK, P], F32, tag="acc", name="acc")
+            x_cols = slice(a * P, (a + 1) * P)
+            for t in range(PACK):
+                w_cols = slice(t * P, (t + 1) * P)
+                nc.tensor.matmul_mx(
+                    out=acc[g][:, t, :],
+                    lhsT=w_codes[:, w_cols].bitcast(FP8X4),
+                    lhsT_scale=w_scales[:, w_cols],
+                    rhs=x_codes[i][:, x_cols].bitcast(FP8X4),
+                    rhs_scale=x_scales[i][:, x_cols],
+                    start=True,
+                    stop=True,
                 )
+
+        def empty_tile(g):
+            i, a = divmod(g, TILES)
+            if a == 0:
+                f_grouped[i] = stage.tile([P, TILES, P, PACK], BF16, tag="f_grouped", name="f_grouped", align_bytes=64)
+            nc.vector.scalar_tensor_tensor(
+                out=f_grouped[i][:, a],
+                in0=acc[g][:].rearrange("p t r -> p r t"),
+                scalar=inv_scale,
+                in1=bias_by_row,
+                op0=ALU.mult,
+                op1=ALU.add,
+            )
 
         def quantise_f(i):
             if i < f1_chunks:
-                codes, scales, c = f1_codes, f1_scales, i
+                cols = slice(i * CHUNK, (i + 1) * CHUNK)
+                codes, scales = f1_codes[:, cols], f1_scales[:, cols]
             else:
-                n, c = divmod(i - f1_chunks, banks)
-                if c == 0:
-                    f0_codes[n] = codes_pool.tile([P, cells0], U32, tag="f0_codes", name="f0_codes", align_bytes=64)
-                    f0_scales[n] = codes_pool.tile([P, cells0], U8, tag="f0_scales", name="f0_scales", align_bytes=64)
-                codes, scales = f0_codes[n], f0_scales[n]
-            cols = slice(c * CHUNK, (c + 1) * CHUNK)
+                f0_codes[i] = to_columns.tile([P, CHUNK], U32, tag="f0_codes", name="f0_codes", align_bytes=64)
+                f0_scales[i] = to_columns.tile([P, CHUNK], U8, tag="f0_scales", name="f0_scales", align_bytes=64)
+                codes, scales = f0_codes[i][:], f0_scales[i][:]
             nc.vector.quantize_mx(
-                out=codes[:, cols].bitcast(FP8X4),
-                scales=scales[:, cols],
-                in_=f_grouped[i][:].rearrange("p a r t -> p (a r t)"),
+                out=codes.bitcast(FP8X4), scales=scales, in_=f_grouped[i][:].rearrange("p a r t -> p (a r t)")
             )
+
+        sim, conf0, sim_in, miss, conf1_t, conf1 = {}, {}, {}, {}, {}, {}
+        row_max, row_sum = {}, {}
+        col_max_bank, col_max_part, col_max_t, col_max, shift1, col_sum = {}, {}, {}, {}, {}, {}
+        recip1_diag, goal1_rep, goal1_bank, goal1_all = {}, {}, {}, {}
+        inv_temp = 1.0 / TEMPERATURE
+
+        def out_chunk(k, i):
+            n, c = batch_and_bank(i)
+            return out[k, n].rearrange("(p j) s -> p j s", j=per_part)[:, c * TILES : (c + 1) * TILES, :]
+
+        def rows_matmul(i):
+            n = batch_and_bank(i)[0]
+            n_cols = slice(n * P, (n + 1) * P)
+            sim[i] = psum_match.tile([P, TILES, P], F32, tag="sim", name="sim")
+            for a in range(TILES):
+                a_cols = slice(a * P, (a + 1) * P)
+                nc.tensor.matmul_mx(
+                    out=sim[i][:, a, :],
+                    lhsT=f0_codes[i][:, a_cols].bitcast(FP8X4),
+                    lhsT_scale=f0_scales[i][:, a_cols],
+                    rhs=f1_codes[:, n_cols].bitcast(FP8X4),
+                    rhs_scale=f1_scales[:, n_cols],
+                    start=True,
+                    stop=True,
+                )
+
+        def rows_maxima(i):
+            n, c = batch_and_bank(i)
+            if c == 0:
+                col_max_bank[n] = by_batch.tile([P, banks, P], F32, tag="col_max_bank", name="col_max_bank")
+            row_max[i] = late.tile([P, TILES], F32, tag="row_max", name="row_max")
+            nc.vector.tensor_reduce(out=row_max[i][:], in_=sim[i][:], axis=AXIS.X, op=ALU.max)
+            nc.vector.tensor_reduce(
+                out=col_max_bank[n][:, c, :], in_=sim[i][:].rearrange("p a s -> p s a"), axis=AXIS.X, op=ALU.max
+            )
+
+        def rows_exp(i):
+            n, c = batch_and_bank(i)
+            shift0 = late.tile([P, TILES], F32, tag="shift0")
+            row_sum[i] = late.tile([P, TILES], F32, tag="row_sum", name="row_sum")
+            conf0[i] = to_mconf.tile([P, TILES, P], F32, tag="conf0", name="conf0")
+            sim_in[i] = to_mconf.tile(shape, F32, tag="sim_in", name="sim_in", bufs=BACK - ROWS + 2)
+            nc.scalar.mul(out=shift0[:], in_=row_max[i][:], mul=-inv_temp)
+            for a in range(TILES):
+                nc.scalar.activation(
+                    out=conf0[i][:, a, :],
+                    in_=sim[i][:, a, :],
+                    func=ACT.Exp,
+                    bias=shift0[:, a : a + 1],
+                    scale=inv_temp,
+                    accum_out=row_sum[i][:, a : a + 1],
+                )
+            for a in range(0, TILES, 2):
+                j = c * TILES + a
+                nc.scalar.activation(
+                    out=sim_in[i][:, a : a + 2],
+                    in_=interior(sim[i][:])[:, a : a + 2],
+                    func=ACT.Identity,
+                    bias=sink[:, j : j + 1],
+                    scale=1.0,
+                )
+
+        def column_maxima_part(n):
+            col_max_part[n] = late.tile([P, P], F32, tag="col_max_part", name="col_max_part")
+            nc.vector.tensor_reduce(
+                out=col_max_part[n][:], in_=col_max_bank[n][:].rearrange("p c s -> p s c"), axis=AXIS.X, op=ALU.max
+            )
+
+        def column_maxima_flip(n):
+            col_max_t[n] = psum_match.tile([P, P], F32, tag="columns", name="col_max_t", bufs=2)
+            nc.tensor.transpose(col_max_t[n][:], col_max_part[n][:], ident[:])
+
+        def column_maxima(n):
+            col_max[n] = by_batch.tile([P, 1], F32, tag="col_max", name="col_max")
+            nc.vector.tensor_reduce(out=col_max[n][:], in_=col_max_t[n][:], axis=AXIS.X, op=ALU.max)
+
+        def column_shift(n):
+            shift1[n] = by_batch.tile([P, 1], F32, tag="shift1", name="shift1")
+            nc.scalar.mul(out=shift1[n][:], in_=col_max[n][:], mul=-inv_temp)
+            col_sum[n] = by_batch.tile([P, banks], F32, tag="col_sum", name="col_sum")
+
+        def finish_rows(i):
+            recip0 = late.tile([P, TILES], F32, tag="recip0")
+            nc.vector.reciprocal(out=recip0[:], in_=row_sum[i][:])
+            for a in range(TILES):
+                nc.scalar.activation(
+                    out=conf0[i][:, a, :], in_=conf0[i][:, a, :], func=ACT.Copy, scale=recip0[:, a : a + 1]
+                )
+            nc.sync.dma_start(out=out_chunk(0, i), in_=conf0[i][:])
+            goal0 = late.tile([P, TILES], F32, tag="goal0")
+            nc.gpsimd.tensor_scalar(out=goal0[:], in0=recip0[:], scalar1=THR, scalar2=FAR, op0=ALU.is_le, op1=ALU.mult)
+            nc.gpsimd.tensor_tensor(out=goal0[:], in0=goal0[:], in1=row_max[i][:], op=ALU.add)
+            miss[i] = to_mconf.tile(shape, F32, tag="miss", name="miss")
+            nc.gpsimd.tensor_tensor(
+                out=miss[i][:],
+                in0=sim_in[i][:],
+                in1=goal0[:].unsqueeze(2).unsqueeze(3).to_broadcast(shape),
+                op=ALU.subtract,
+            )
+
+        def row_signs(i):
+            nc.scalar.activation(out=miss[i][:], in_=miss[i][:], func=ACT.Sign)
+
+        def columns_matmul(i):
+            n = batch_and_bank(i)[0]
+            n_cols = slice(n * P, (n + 1) * P)
+            sim_t = psum_flip.tile([P, CHUNK], F32, tag="flipped")
+            nc.tensor.matmul_mx(
+                out=sim_t[:],
+                lhsT=f1_codes[:, n_cols].bitcast(FP8X4),
+                lhsT_scale=f1_scales[:, n_cols],
+                rhs=f0_codes[i][:].bitcast(FP8X4),
+                rhs_scale=f0_scales[i][:],
+                start=True,
+                stop=True,
+            )
+            return sim_t
+
+        def columns_exp(i, sim_t):
+            n, c = batch_and_bank(i)
+            conf1_t[i] = to_back.tile([P, CHUNK], F32, tag="conf1_t", name="conf1_t")
+            nc.scalar.activation(
+                out=conf1_t[i][:],
+                in_=sim_t[:],
+                func=ACT.Exp,
+                bias=shift1[n][:],
+                scale=inv_temp,
+                accum_out=col_sum[n][:, c : c + 1],
+            )
+
+        def batch_sums(n):
+            recip1 = late.tile([P, 1], F32, tag="recip1")
+            nc.vector.tensor_reduce(out=recip1[:], in_=col_sum[n][:], axis=AXIS.X, op=ALU.add)
+            nc.vector.reciprocal(out=recip1[:], in_=recip1[:])
+            recip1_diag[n] = by_batch.tile([P, P], F32, tag="recip1_diag", name="recip1_diag")
+            nc.vector.tensor_scalar_mul(out=recip1_diag[n][:], in0=ident[:], scalar1=recip1[:])
+            goal1 = late.tile([P, 1], F32, tag="goal1")
+            nc.vector.tensor_scalar(out=goal1[:], in0=recip1[:], scalar1=THR, scalar2=FAR, op0=ALU.is_le, op1=ALU.mult)
+            nc.vector.tensor_tensor(out=goal1[:], in0=goal1[:], in1=col_max[n][:], op=ALU.add)
+            goal1_rep[n] = late.tile([P, P], F32, tag="goal1_rep", name="goal1_rep")
+            nc.vector.tensor_copy(out=goal1_rep[n][:], in_=goal1[:].to_broadcast([P, P]))
+
+        def goal1_flip(n):
+            goal1_bank[n] = psum_match.tile([P, P], F32, tag="columns", name="goal1_bank", bufs=2)
+            nc.tensor.transpose(goal1_bank[n][:], goal1_rep[n][:], ident[:])
+
+        def goal1_copy(n):
+            goal1_all[n] = by_batch.tile([P, 1, P], F32, tag="goal1_all", name="goal1_all")
+            nc.scalar.copy(out=goal1_all[n][:, 0, :], in_=goal1_bank[n][:])
+
+        def back_matmul(i):
+            n = batch_and_bank(i)[0]
+            conf1_bank = psum_match.tile([P, TILES, P], F32, tag="columns", bufs=2)
+            for a in range(TILES):
+                nc.tensor.matmul(
+                    out=conf1_bank[:, a, :],
+                    lhsT=conf1_t[i][:, a * P : (a + 1) * P],
+                    rhs=recip1_diag[n][:],
+                    start=True,
+                    stop=True,
+                )
+            return conf1_bank
+
+        def back_copy(i, conf1_bank):
+            n = batch_and_bank(i)[0]
+            conf1[i] = late.tile([P, TILES, P], F32, tag="conf1", name="conf1", bufs=MCONF - BACK + 2)
+            nc.scalar.copy(out=conf1[i][:], in_=conf1_bank[:])
+            nc.sync.dma_start(out=out_chunk(1, i), in_=conf1[i][:])
+            gap1 = late.tile(shape, F32, tag="gap1")
+            nc.gpsimd.tensor_tensor(
+                out=gap1[:], in0=sim_in[i][:], in1=interior(goal1_all[n][:]).to_broadcast(shape), op=ALU.subtract
+            )
+            nc.gpsimd.tensor_tensor(out=miss[i][:], in0=miss[i][:], in1=gap1[:], op=ALU.mult)
+
+        def mconf_chunk(i):
+            larger = late.tile(shape, F32, tag="larger")
+            nc.vector.tensor_tensor(out=larger[:], in0=interior(conf0[i][:]), in1=interior(conf1[i][:]), op=ALU.max)
+            mconf = mconf_tiles[i % len(mconf_tiles)]
+            for a in range(TILES):
+                nc.vector.scalar_tensor_tensor(
+                    out=interior(mconf[:])[:, a],
+                    in0=miss[i][:, a],
+                    scalar=0.0,
+                    in1=larger[:, a],
+                    op0=ALU.is_equal,
+                    op1=ALU.mult,
+                )
+            nc.sync.dma_start(out=out_chunk(2, i), in_=mconf[:])
 
         w_rows = keep.tile([P, PACK * FEAT], BF16)
         nc.sync.dma_start(out=w_rows[:], in_=W.rearrange("(p t) k -> p (t k)", t=PACK))
         f1_rows = keep.tile([P, batches * FEAT], BF16)
-        nc.sync.dma_start(
-            out=f1_rows[:].rearrange("s (n k) -> s n k", n=batches), in_=feat_c1.rearrange("n s k -> s n k")
-        )
+        for i in range(batches // TILES):
+            nc.sync.dma_start(
+                out=f1_rows[:, i * TILES * FEAT : (i + 1) * TILES * FEAT].rearrange("s (n k) -> s n k", n=TILES),
+                in_=feat_c1[i * TILES : (i + 1) * TILES].rearrange("n s k -> s n k"),
+            )
         b_raw = keep.tile([P, PACK], BF16)
         nc.sync.dma_start(out=b_raw[:], in_=b.rearrange("(p t) -> p t", t=PACK))
         load_batch(0)
@@ -182,8 +396,6 @@ def tile_coarsematching_t_kernel(tc, feat_c0, feat_c1, W, b, h0c, w0c, h1c, w1c,
 
         w_codes = keep.tile([P, FEAT], U32, align_bytes=64)
         w_scales = keep.tile([P, FEAT], U8, align_bytes=64)
-        w_grouped = flip_rows(w_rows[:])
-        nc.vector.quantize_mx(out=w_codes[:].bitcast(FP8X4), scales=w_scales[:], in_=w_grouped[:])
         f1_codes = keep.tile([P, batches * P], U32, align_bytes=64)
         f1_scales = keep.tile([P, batches * P], U8, align_bytes=64)
 
@@ -192,185 +404,72 @@ def tile_coarsematching_t_kernel(tc, feat_c0, feat_c1, W, b, h0c, w0c, h1c, w1c,
         nc.vector.tensor_single_scalar(out=bias[:], in_=b_raw[:], scalar=inv_scale, op=ALU.mult)
         bias_by_row = bias[:].unsqueeze(1).to_broadcast([P, P, PACK])
 
-        live = {}
-        inv_temp = 1.0 / TEMPERATURE
-
-        def by_cell(per_cell):
-            return per_cell.unsqueeze(2).unsqueeze(3).to_broadcast(shape)
-
-        def out_plane(k, n):
-            return out[k, n].rearrange("(p j) s -> p j s", j=per_part)
-
-        def rows_chunk(n, c):
-            if c == 0:
-                live["row_max", n] = small.tile([P, per_part], F32, tag="row_max", name="row_max")
-                live["shift0", n] = small.tile([P, per_part], F32, tag="shift0", name="shift0")
-                live["row_sum", n] = small.tile([P, per_part], F32, tag="row_sum", name="row_sum")
-                live["col_max_bank", n] = small.tile([P, banks, P], F32, tag="col_max_bank", name="col_max_bank")
-                live["conf0", n] = planes.tile([P, per_part, P], F32, tag="conf0", name="conf0")
-                live["sim_in", n] = planes.tile(shape, F32, tag="sim_in", name="sim_in")
-            row_max, shift0, row_sum = live["row_max", n], live["shift0", n], live["row_sum", n]
-            n_cols = slice(n * P, (n + 1) * P)
-            sim = psum_match.tile([P, TILES, P], F32, tag="match")
-            for a in range(TILES):
-                j_cols = slice((c * TILES + a) * P, (c * TILES + a + 1) * P)
-                nc.tensor.matmul_mx(
-                    out=sim[:, a, :],
-                    lhsT=f0_codes[n][:, j_cols].bitcast(FP8X4),
-                    lhsT_scale=f0_scales[n][:, j_cols],
-                    rhs=f1_codes[:, n_cols].bitcast(FP8X4),
-                    rhs_scale=f1_scales[:, n_cols],
-                    start=True,
-                    stop=True,
-                )
-            js = slice(c * TILES, (c + 1) * TILES)
-            nc.vector.tensor_reduce(out=row_max[:, js], in_=sim[:], axis=AXIS.X, op=ALU.max)
-            nc.vector.tensor_reduce(
-                out=live["col_max_bank", n][:, c, :], in_=sim[:].rearrange("p a s -> p s a"), axis=AXIS.X, op=ALU.max
-            )
-            nc.scalar.mul(out=shift0[:, js], in_=row_max[:, js], mul=-inv_temp)
-            for a in range(TILES):
-                j = c * TILES + a
-                nc.scalar.activation(
-                    out=live["conf0", n][:, j, :],
-                    in_=sim[:, a, :],
-                    func=ACT.Exp,
-                    bias=shift0[:, j : j + 1],
-                    scale=inv_temp,
-                    accum_out=row_sum[:, j : j + 1],
-                )
-            nc.scalar.copy(out=live["sim_in", n][:, js], in_=interior(sim[:]))
-
-        def column_maxima(n):
-            col_max_part = small.tile([P, P], F32, tag="col_max_part")
-            nc.vector.tensor_reduce(
-                out=col_max_part[:],
-                in_=live["col_max_bank", n][:].rearrange("p c s -> p s c"),
-                axis=AXIS.X,
-                op=ALU.max,
-            )
-            col_max_t = psum_flip.tile([P, P], F32, tag="flipped")
-            nc.tensor.transpose(col_max_t[:], col_max_part[:], ident[:])
-            live["col_max_t", n] = col_max_t
-
-        def phase_columns(n):
-            n_cols = slice(n * P, (n + 1) * P)
-            conf0 = live["conf0", n]
-            col_max = small.tile([P, 1], F32, tag="col_max")
-            nc.vector.tensor_reduce(out=col_max[:], in_=live["col_max_t", n][:], axis=AXIS.X, op=ALU.max)
-            shift1 = small.tile([P, 1], F32, tag="shift1")
-            nc.scalar.mul(out=shift1[:], in_=col_max[:], mul=-inv_temp)
-            recip0 = small.tile([P, per_part], F32, tag="recip0")
-            nc.vector.reciprocal(out=recip0[:], in_=live["row_sum", n][:])
-            conf1_t = planes.tile([P, cells0], F32, tag="conf1_t")
-            col_sum = small.tile([P, banks], F32, tag="col_sum")
-            for c in range(banks):
-                cols = slice(c * CHUNK, (c + 1) * CHUNK)
-                sim_t = psum_match.tile([P, CHUNK], F32, tag="match")
-                nc.tensor.matmul_mx(
-                    out=sim_t[:],
-                    lhsT=f1_codes[:, n_cols].bitcast(FP8X4),
-                    lhsT_scale=f1_scales[:, n_cols],
-                    rhs=f0_codes[n][:, cols].bitcast(FP8X4),
-                    rhs_scale=f0_scales[n][:, cols],
-                    start=True,
-                    stop=True,
-                )
-                nc.scalar.activation(
-                    out=conf1_t[:, cols],
-                    in_=sim_t[:],
-                    func=ACT.Exp,
-                    bias=shift1[:],
-                    scale=inv_temp,
-                    accum_out=col_sum[:, c : c + 1],
-                )
-            for j in range(per_part):
-                nc.scalar.activation(out=conf0[:, j, :], in_=conf0[:, j, :], func=ACT.Copy, scale=recip0[:, j : j + 1])
-            nc.sync.dma_start(out=out_plane(0, n), in_=conf0[:])
-            goal0 = small.tile([P, per_part], F32, tag="goal0")
-            nc.gpsimd.tensor_scalar(out=goal0[:], in0=recip0[:], scalar1=THR, scalar2=FAR, op0=ALU.is_le, op1=ALU.mult)
-            nc.gpsimd.tensor_tensor(out=goal0[:], in0=goal0[:], in1=live["row_max", n][:], op=ALU.add)
-            miss = planes.tile(shape, F32, tag="miss")
-            nc.gpsimd.tensor_tensor(out=miss[:], in0=live["sim_in", n][:], in1=by_cell(goal0[:]), op=ALU.subtract)
-            nc.scalar.activation(out=miss[:], in_=miss[:], func=ACT.Sign)
-            live["col_max", n], live["col_sum", n], live["conf1_t", n], live["miss", n] = col_max, col_sum, conf1_t, miss
-
-        def phase_back(n):
-            conf1_t, miss = live["conf1_t", n], live["miss", n]
-            recip1 = small.tile([P, 1], F32, tag="recip1")
-            nc.vector.tensor_reduce(out=recip1[:], in_=live["col_sum", n][:], axis=AXIS.X, op=ALU.add)
-            nc.vector.reciprocal(out=recip1[:], in_=recip1[:])
-            recip1_diag = small.tile([P, P], F32, tag="recip1_diag")
-            nc.vector.tensor_scalar_mul(out=recip1_diag[:], in0=ident[:], scalar1=recip1[:])
-            goal1 = small.tile([P, 1], F32, tag="goal1")
-            nc.vector.tensor_scalar(out=goal1[:], in0=recip1[:], scalar1=THR, scalar2=FAR, op0=ALU.is_le, op1=ALU.mult)
-            nc.vector.tensor_tensor(out=goal1[:], in0=goal1[:], in1=live["col_max", n][:], op=ALU.add)
-            goal1_rep = small.tile([P, P], F32, tag="goal1_rep")
-            nc.vector.tensor_copy(out=goal1_rep[:], in_=goal1[:].to_broadcast([P, P]))
-            goal1_bank = psum_flip.tile([P, P], F32, tag="flipped")
-            nc.tensor.transpose(goal1_bank[:], goal1_rep[:], ident[:])
-            goal1_all = small.tile([P, 1, P], F32, tag="goal1_all")
-            nc.scalar.copy(out=goal1_all[:, 0, :], in_=goal1_bank[:])
-            conf1 = planes.tile([P, per_part, P], F32, tag="conf1")
-            for c in range(banks):
-                conf1_bank = psum_match.tile([P, TILES, P], F32, tag="match")
-                for a in range(TILES):
-                    j = c * TILES + a
-                    nc.tensor.matmul(
-                        out=conf1_bank[:, a, :],
-                        lhsT=conf1_t[:, j * P : (j + 1) * P],
-                        rhs=recip1_diag[:],
-                        start=True,
-                        stop=True,
-                    )
-                nc.scalar.copy(out=conf1[:, c * TILES : (c + 1) * TILES, :], in_=conf1_bank[:])
-            nc.sync.dma_start(out=out_plane(1, n), in_=conf1[:])
-            gap1 = planes.tile(shape, F32, tag="gap1")
-            nc.gpsimd.tensor_tensor(
-                out=gap1[:], in0=live["sim_in", n][:], in1=interior(goal1_all[:]).to_broadcast(shape), op=ALU.subtract
-            )
-            nc.gpsimd.tensor_tensor(out=miss[:], in0=miss[:], in1=gap1[:], op=ALU.mult)
-            live["conf1", n] = conf1
-
-        def phase_mconf(n):
-            larger = planes.tile(shape, F32, tag="larger")
-            nc.vector.tensor_tensor(
-                out=larger[:], in0=interior(live["conf0", n][:]), in1=interior(live["conf1", n][:]), op=ALU.max
-            )
-            nc.vector.scalar_tensor_tensor(
-                out=larger[:].rearrange("p j r c -> p (j r c)"),
-                in0=live["miss", n][:].rearrange("p j r c -> p (j r c)"),
-                scalar=0.0,
-                in1=larger[:].rearrange("p j r c -> p (j r c)"),
-                op0=ALU.is_equal,
-                op1=ALU.mult,
-            )
-            mconf = mconf_tiles[n % 2]
-            nc.gpsimd.tensor_tensor(out=interior(mconf[:]), in0=larger[:], in1=by_cell(inside[:]), op=ALU.mult)
-            nc.sync.dma_start(out=out_plane(2, n), in_=mconf[:])
-
-        phases = [phase_columns, phase_back, phase_mconf]
+        ctx.enter_context(tc.manual_schedule())
+        w_grouped = flip_rows(w_rows[:])
         flip(0)
+        nc.vector.quantize_mx(out=w_codes[:].bitcast(FP8X4), scales=w_scales[:], in_=w_grouped[:])
         flip(1)
         quantise_x(0)
-        for i in range(n_chunks + 2 + PHASE_GAP * (len(phases) - 1)):
+        for g in range(LEAD):
+            project_tile(g)
+
+        def last_of_batch(i):
+            if is_f0_chunk(i) and batch_and_bank(i)[1] == banks - 1:
+                return batch_and_bank(i)[0]
+            return None
+
+        for i in range(n_chunks + MCONF):
             n, c = divmod(i, banks)
             if c == 0 and n + 2 < batches:
                 load_batch(n + 2)
-            if 1 <= i <= n_chunks:
-                quantise_f(i - 1)
-            if i < n_chunks:
-                project(i)
-            if i + 2 < n_chunks:
-                flip(i + 2)
-            if i + 1 < n_chunks:
-                quantise_x(i + 1)
-            for k in reversed(range(len(phases))):
-                n, c = divmod(i - 2 - PHASE_GAP * k - f1_chunks, banks)
-                if c == banks - 1 and 0 <= n < batches:
-                    phases[k](n)
-            n, c = divmod(i - 1 - f1_chunks, banks)
-            if 0 <= n < batches:
-                rows_chunk(n, c)
-                if c == banks - 1:
-                    column_maxima(n)
+            maxima_due = last_of_batch(i - ROWS - 1)
+            sums_due = last_of_batch(i - COLUMNS - 1)
+            for slot in range(TILES):
+                g = i * TILES + slot
+                if is_chunk((g + LEAD) // TILES):
+                    project_tile(g + LEAD)
+                if is_chunk(i - PROJECT):
+                    empty_tile(g)
+                if slot == 0:
+                    if is_chunk(i - ROWS):
+                        quantise_f(i - ROWS)
+                    if maxima_due is not None:
+                        column_maxima_flip(maxima_due)
+                    if is_chunk(i - FLIP):
+                        flip(i - FLIP)
+                if slot == 1:
+                    if is_chunk(i - QUANTISE_X):
+                        quantise_x(i - QUANTISE_X)
+                    if is_f0_chunk(i - ROWS):
+                        rows_matmul(i - ROWS)
+                    if maxima_due is not None:
+                        column_maxima(maxima_due)
+                        column_shift(maxima_due)
+                    if is_f0_chunk(i - COLUMNS):
+                        sim_t = columns_matmul(i - COLUMNS)
+                    if is_f0_chunk(i - FINISH_ROWS):
+                        finish_rows(i - FINISH_ROWS)
+                    if sums_due is not None:
+                        batch_sums(sums_due)
+                if slot == 2:
+                    if is_f0_chunk(i - ROWS):
+                        rows_maxima(i - ROWS)
+                    if is_f0_chunk(i - COLUMNS):
+                        columns_exp(i - COLUMNS, sim_t)
+                    if sums_due is not None:
+                        goal1_flip(sums_due)
+                    if is_f0_chunk(i - BACK):
+                        conf1_bank = back_matmul(i - BACK)
+                if slot == 3:
+                    if is_f0_chunk(i - ROWS):
+                        rows_exp(i - ROWS)
+                    if sums_due is not None:
+                        goal1_copy(sums_due)
+                    if is_f0_chunk(i - BACK):
+                        back_copy(i - BACK, conf1_bank)
+                    if is_f0_chunk(i - FINISH_ROWS):
+                        row_signs(i - FINISH_ROWS)
+                    if last_of_batch(i - ROWS) is not None:
+                        column_maxima_part(last_of_batch(i - ROWS))
+                    if is_f0_chunk(i - MCONF):
+                        mconf_chunk(i - MCONF)

@@ -31,7 +31,8 @@ ROWS = 1
 FINISH_ROWS = 2
 COLUMNS = 4
 BACK = 7
-MCONF = 8
+GAPS = 8
+MCONF = 9
 LEAD = 2
 
 FLOPS = 2 * (8 * 1536 + 8 * 128) * 512 * 512 + 2 * 8 * 1536 * 128 * 512
@@ -118,12 +119,12 @@ def tile_coarsematching_t_kernel(tc, feat_c0, feat_c1, W, b, h0c, w0c, h1c, w1c,
         def batch_and_bank(i):
             return divmod(i - f1_chunks, banks)
 
-        def flip_rows(rows):
+        def flip_rows(rows, bank_pool, bank_tag):
             words = rows.bitcast(F32)
             grouped = stage.tile([P, CHUNK * PACK], BF16, tag="x_grouped", align_bytes=64)
             grouped_words = grouped[:].bitcast(F32).rearrange("q (a r u) -> q a r u", a=TILES, u=2)
             for pair in range(TILES // 2):
-                flipped = psum_flip.tile([P, 2, 2, P], F32, tag="flipped")
+                flipped = bank_pool.tile([P, 2, 2, P], F32, tag=bank_tag, name="flipped")
                 for a in range(2):
                     for u in range(2):
                         first = ((2 * pair + a) * 2 + u) * P
@@ -144,12 +145,19 @@ def tile_coarsematching_t_kernel(tc, feat_c0, feat_c1, W, b, h0c, w0c, h1c, w1c,
             else:
                 n, c = batch_and_bank(i)
                 rows = f0_rows[n][:, c * chunk_elems : (c + 1) * chunk_elems]
-            x_grouped[i] = flip_rows(rows)
+            x_grouped[i] = flip_rows(rows, psum_flip, "flipped")
 
-        def quantise_x(i):
+        def quantise_x(i, pieces=1):
             x_codes[i] = stage.tile([P, CHUNK], U32, tag="x_codes", name="x_codes", align_bytes=64)
             x_scales[i] = stage.tile([P, CHUNK], U8, tag="x_scales", name="x_scales", align_bytes=64)
-            nc.vector.quantize_mx(out=x_codes[i][:].bitcast(FP8X4), scales=x_scales[i][:], in_=x_grouped[i][:])
+            width = CHUNK // pieces
+            for piece in range(pieces):
+                cols = slice(piece * width, (piece + 1) * width)
+                nc.vector.quantize_mx(
+                    out=x_codes[i][:, cols].bitcast(FP8X4),
+                    scales=x_scales[i][:, cols],
+                    in_=x_grouped[i][:, piece * width * PACK : (piece + 1) * width * PACK],
+                )
 
         def project_tile(g):
             i, a = divmod(g, TILES)
@@ -193,7 +201,7 @@ def tile_coarsematching_t_kernel(tc, feat_c0, feat_c1, W, b, h0c, w0c, h1c, w1c,
             )
 
         sim, conf0, sim_in, miss, conf1_t, conf1 = {}, {}, {}, {}, {}, {}
-        row_max, row_sum = {}, {}
+        row_max, row_sum, recip0 = {}, {}, {}
         col_max_bank, col_max_part, col_max_t, col_max, shift1, col_sum = {}, {}, {}, {}, {}, {}
         recip1_diag, goal1_rep, goal1_bank, goal1_all = {}, {}, {}, {}
         inv_temp = 1.0 / TEMPERATURE
@@ -218,12 +226,14 @@ def tile_coarsematching_t_kernel(tc, feat_c0, feat_c1, W, b, h0c, w0c, h1c, w1c,
                     stop=True,
                 )
 
-        def rows_maxima(i):
+        def row_maxima(i):
+            row_max[i] = late.tile([P, TILES], F32, tag="row_max", name="row_max")
+            nc.vector.tensor_reduce(out=row_max[i][:], in_=sim[i][:], axis=AXIS.X, op=ALU.max)
+
+        def column_maxima_chunk(i):
             n, c = batch_and_bank(i)
             if c == 0:
                 col_max_bank[n] = by_batch.tile([P, banks, P], F32, tag="col_max_bank", name="col_max_bank")
-            row_max[i] = late.tile([P, TILES], F32, tag="row_max", name="row_max")
-            nc.vector.tensor_reduce(out=row_max[i][:], in_=sim[i][:], axis=AXIS.X, op=ALU.max)
             nc.vector.tensor_reduce(
                 out=col_max_bank[n][:, c, :], in_=sim[i][:].rearrange("p a s -> p s a"), axis=AXIS.X, op=ALU.max
             )
@@ -233,7 +243,7 @@ def tile_coarsematching_t_kernel(tc, feat_c0, feat_c1, W, b, h0c, w0c, h1c, w1c,
             shift0 = late.tile([P, TILES], F32, tag="shift0")
             row_sum[i] = late.tile([P, TILES], F32, tag="row_sum", name="row_sum")
             conf0[i] = to_mconf.tile([P, TILES, P], F32, tag="conf0", name="conf0")
-            sim_in[i] = to_mconf.tile(shape, F32, tag="sim_in", name="sim_in", bufs=BACK - ROWS + 2)
+            sim_in[i] = to_mconf.tile(shape, F32, tag="sim_in", name="sim_in", bufs=GAPS - ROWS + 2)
             nc.scalar.mul(out=shift0[:], in_=row_max[i][:], mul=-inv_temp)
             for a in range(TILES):
                 nc.scalar.activation(
@@ -273,16 +283,18 @@ def tile_coarsematching_t_kernel(tc, feat_c0, feat_c1, W, b, h0c, w0c, h1c, w1c,
             nc.scalar.mul(out=shift1[n][:], in_=col_max[n][:], mul=-inv_temp)
             col_sum[n] = by_batch.tile([P, banks], F32, tag="col_sum", name="col_sum")
 
-        def finish_rows(i):
-            recip0 = late.tile([P, TILES], F32, tag="recip0")
-            nc.vector.reciprocal(out=recip0[:], in_=row_sum[i][:])
+        def finish_conf0(i):
             for a in range(TILES):
                 nc.scalar.activation(
-                    out=conf0[i][:, a, :], in_=conf0[i][:, a, :], func=ACT.Copy, scale=recip0[:, a : a + 1]
+                    out=conf0[i][:, a, :], in_=conf0[i][:, a, :], func=ACT.Copy, scale=recip0[i][:, a : a + 1]
                 )
             nc.sync.dma_start(out=out_chunk(0, i), in_=conf0[i][:])
+
+        def row_goals(i):
+            recip0[i] = late.tile([P, TILES], F32, tag="recip0", name="recip0")
+            nc.vector.reciprocal(out=recip0[i][:], in_=row_sum[i][:])
             goal0 = late.tile([P, TILES], F32, tag="goal0")
-            nc.gpsimd.tensor_scalar(out=goal0[:], in0=recip0[:], scalar1=THR, scalar2=FAR, op0=ALU.is_le, op1=ALU.mult)
+            nc.gpsimd.tensor_scalar(out=goal0[:], in0=recip0[i][:], scalar1=THR, scalar2=FAR, op0=ALU.is_le, op1=ALU.mult)
             nc.gpsimd.tensor_tensor(out=goal0[:], in0=goal0[:], in1=row_max[i][:], op=ALU.add)
             miss[i] = to_mconf.tile(shape, F32, tag="miss", name="miss")
             nc.gpsimd.tensor_tensor(
@@ -356,10 +368,12 @@ def tile_coarsematching_t_kernel(tc, feat_c0, feat_c1, W, b, h0c, w0c, h1c, w1c,
             return conf1_bank
 
         def back_copy(i, conf1_bank):
-            n = batch_and_bank(i)[0]
             conf1[i] = late.tile([P, TILES, P], F32, tag="conf1", name="conf1", bufs=MCONF - BACK + 2)
             nc.scalar.copy(out=conf1[i][:], in_=conf1_bank[:])
             nc.sync.dma_start(out=out_chunk(1, i), in_=conf1[i][:])
+
+        def gaps(i):
+            n = batch_and_bank(i)[0]
             gap1 = late.tile(shape, F32, tag="gap1")
             nc.gpsimd.tensor_tensor(
                 out=gap1[:], in0=sim_in[i][:], in1=interior(goal1_all[n][:]).to_broadcast(shape), op=ALU.subtract
@@ -405,11 +419,11 @@ def tile_coarsematching_t_kernel(tc, feat_c0, feat_c1, W, b, h0c, w0c, h1c, w1c,
         bias_by_row = bias[:].unsqueeze(1).to_broadcast([P, P, PACK])
 
         ctx.enter_context(tc.manual_schedule())
-        w_grouped = flip_rows(w_rows[:])
+        w_grouped = flip_rows(w_rows[:], psum_proj, "acc")
         flip(0)
         nc.vector.quantize_mx(out=w_codes[:].bitcast(FP8X4), scales=w_scales[:], in_=w_grouped[:])
+        quantise_x(0, pieces=2)
         flip(1)
-        quantise_x(0)
         for g in range(LEAD):
             project_tile(g)
 
@@ -433,13 +447,13 @@ def tile_coarsematching_t_kernel(tc, feat_c0, feat_c1, W, b, h0c, w0c, h1c, w1c,
                 if slot == 0:
                     if is_chunk(i - ROWS):
                         quantise_f(i - ROWS)
+                    if is_chunk(i - QUANTISE_X):
+                        quantise_x(i - QUANTISE_X)
                     if maxima_due is not None:
                         column_maxima_flip(maxima_due)
                     if is_chunk(i - FLIP):
                         flip(i - FLIP)
                 if slot == 1:
-                    if is_chunk(i - QUANTISE_X):
-                        quantise_x(i - QUANTISE_X)
                     if is_f0_chunk(i - ROWS):
                         rows_matmul(i - ROWS)
                     if maxima_due is not None:
@@ -447,21 +461,28 @@ def tile_coarsematching_t_kernel(tc, feat_c0, feat_c1, W, b, h0c, w0c, h1c, w1c,
                         column_shift(maxima_due)
                     if is_f0_chunk(i - COLUMNS):
                         sim_t = columns_matmul(i - COLUMNS)
-                    if is_f0_chunk(i - FINISH_ROWS):
-                        finish_rows(i - FINISH_ROWS)
                     if sums_due is not None:
                         batch_sums(sums_due)
+                    if is_f0_chunk(i - MCONF):
+                        mconf_chunk(i - MCONF)
+                    if is_f0_chunk(i - FINISH_ROWS):
+                        row_goals(i - FINISH_ROWS)
+                    if is_f0_chunk(i - GAPS):
+                        gaps(i - GAPS)
                 if slot == 2:
                     if is_f0_chunk(i - ROWS):
-                        rows_maxima(i - ROWS)
+                        row_maxima(i - ROWS)
                     if is_f0_chunk(i - COLUMNS):
                         columns_exp(i - COLUMNS, sim_t)
+                    if is_f0_chunk(i - FINISH_ROWS):
+                        finish_conf0(i - FINISH_ROWS)
                     if sums_due is not None:
                         goal1_flip(sums_due)
                     if is_f0_chunk(i - BACK):
                         conf1_bank = back_matmul(i - BACK)
                 if slot == 3:
                     if is_f0_chunk(i - ROWS):
+                        column_maxima_chunk(i - ROWS)
                         rows_exp(i - ROWS)
                     if sums_due is not None:
                         goal1_copy(sums_due)
@@ -471,5 +492,3 @@ def tile_coarsematching_t_kernel(tc, feat_c0, feat_c1, W, b, h0c, w0c, h1c, w1c,
                         row_signs(i - FINISH_ROWS)
                     if last_of_batch(i - ROWS) is not None:
                         column_maxima_part(last_of_batch(i - ROWS))
-                    if is_f0_chunk(i - MCONF):
-                        mconf_chunk(i - MCONF)

@@ -202,7 +202,7 @@ def tile_coarsematching_t_kernel(tc, feat_c0, feat_c1, W, b, h0c, w0c, h1c, w1c,
 
         sim, conf0, sim_in, miss, conf1_t, conf1 = {}, {}, {}, {}, {}, {}
         row_max, row_sum, recip0 = {}, {}, {}
-        col_max_bank, col_max_part, col_max_t, col_max, shift1, col_sum = {}, {}, {}, {}, {}, {}
+        sim_t_early, col_max_chunks, col_max, shift1, col_sum = {}, {}, {}, {}, {}
         recip1_diag, goal1_rep, goal1_bank, goal1_all = {}, {}, {}, {}
         inv_temp = 1.0 / TEMPERATURE
 
@@ -233,10 +233,8 @@ def tile_coarsematching_t_kernel(tc, feat_c0, feat_c1, W, b, h0c, w0c, h1c, w1c,
         def column_maxima_chunk(i):
             n, c = batch_and_bank(i)
             if c == 0:
-                col_max_bank[n] = by_batch.tile([P, banks, P], F32, tag="col_max_bank", name="col_max_bank")
-            nc.vector.tensor_reduce(
-                out=col_max_bank[n][:, c, :], in_=sim[i][:].rearrange("p a s -> p s a"), axis=AXIS.X, op=ALU.max
-            )
+                col_max_chunks[n] = by_batch.tile([P, banks], F32, tag="col_max_chunks", name="col_max_chunks")
+            nc.vector.tensor_reduce(out=col_max_chunks[n][:, c : c + 1], in_=sim_t_early[i][:], axis=AXIS.X, op=ALU.max)
 
         def rows_exp(i):
             n, c = batch_and_bank(i)
@@ -264,19 +262,9 @@ def tile_coarsematching_t_kernel(tc, feat_c0, feat_c1, W, b, h0c, w0c, h1c, w1c,
                     scale=1.0,
                 )
 
-        def column_maxima_part(n):
-            col_max_part[n] = late.tile([P, P], F32, tag="col_max_part", name="col_max_part")
-            nc.vector.tensor_reduce(
-                out=col_max_part[n][:], in_=col_max_bank[n][:].rearrange("p c s -> p s c"), axis=AXIS.X, op=ALU.max
-            )
-
-        def column_maxima_flip(n):
-            col_max_t[n] = psum_match.tile([P, P], F32, tag="columns", name="col_max_t", bufs=2)
-            nc.tensor.transpose(col_max_t[n][:], col_max_part[n][:], ident[:])
-
         def column_maxima(n):
             col_max[n] = by_batch.tile([P, 1], F32, tag="col_max", name="col_max")
-            nc.vector.tensor_reduce(out=col_max[n][:], in_=col_max_t[n][:], axis=AXIS.X, op=ALU.max)
+            nc.vector.tensor_reduce(out=col_max[n][:], in_=col_max_chunks[n][:], axis=AXIS.X, op=ALU.max)
 
         def column_shift(n):
             shift1[n] = by_batch.tile([P, 1], F32, tag="shift1", name="shift1")
@@ -307,10 +295,9 @@ def tile_coarsematching_t_kernel(tc, feat_c0, feat_c1, W, b, h0c, w0c, h1c, w1c,
         def row_signs(i):
             nc.scalar.activation(out=miss[i][:], in_=miss[i][:], func=ACT.Sign)
 
-        def columns_matmul(i):
+        def columns_matmul(i, sim_t):
             n = batch_and_bank(i)[0]
             n_cols = slice(n * P, (n + 1) * P)
-            sim_t = psum_flip.tile([P, CHUNK], F32, tag="flipped")
             nc.tensor.matmul_mx(
                 out=sim_t[:],
                 lhsT=f1_codes[:, n_cols].bitcast(FP8X4),
@@ -320,7 +307,6 @@ def tile_coarsematching_t_kernel(tc, feat_c0, feat_c1, W, b, h0c, w0c, h1c, w1c,
                 start=True,
                 stop=True,
             )
-            return sim_t
 
         def columns_exp(i, sim_t):
             n, c = batch_and_bank(i)
@@ -347,7 +333,7 @@ def tile_coarsematching_t_kernel(tc, feat_c0, feat_c1, W, b, h0c, w0c, h1c, w1c,
             nc.vector.tensor_copy(out=goal1_rep[n][:], in_=goal1[:].to_broadcast([P, P]))
 
         def goal1_flip(n):
-            goal1_bank[n] = psum_match.tile([P, P], F32, tag="columns", name="goal1_bank", bufs=2)
+            goal1_bank[n] = psum_flip.tile([P, P], F32, tag="flipped", name="goal1_bank")
             nc.tensor.transpose(goal1_bank[n][:], goal1_rep[n][:], ident[:])
 
         def goal1_copy(n):
@@ -418,7 +404,6 @@ def tile_coarsematching_t_kernel(tc, feat_c0, feat_c1, W, b, h0c, w0c, h1c, w1c,
         nc.vector.tensor_single_scalar(out=bias[:], in_=b_raw[:], scalar=inv_scale, op=ALU.mult)
         bias_by_row = bias[:].unsqueeze(1).to_broadcast([P, P, PACK])
 
-        ctx.enter_context(tc.manual_schedule())
         w_grouped = flip_rows(w_rows[:], psum_proj, "acc")
         flip(0)
         nc.vector.quantize_mx(out=w_codes[:].bitcast(FP8X4), scales=w_scales[:], in_=w_grouped[:])
@@ -449,18 +434,18 @@ def tile_coarsematching_t_kernel(tc, feat_c0, feat_c1, W, b, h0c, w0c, h1c, w1c,
                         quantise_f(i - ROWS)
                     if is_chunk(i - QUANTISE_X):
                         quantise_x(i - QUANTISE_X)
-                    if maxima_due is not None:
-                        column_maxima_flip(maxima_due)
                     if is_chunk(i - FLIP):
                         flip(i - FLIP)
                 if slot == 1:
                     if is_f0_chunk(i - ROWS):
                         rows_matmul(i - ROWS)
+                        sim_t_early[i - ROWS] = psum_match.tile([P, CHUNK], F32, tag="columns", name="sim_t_early", bufs=2)
+                        columns_matmul(i - ROWS, sim_t_early[i - ROWS])
                     if maxima_due is not None:
-                        column_maxima(maxima_due)
                         column_shift(maxima_due)
                     if is_f0_chunk(i - COLUMNS):
-                        sim_t = columns_matmul(i - COLUMNS)
+                        sim_t = psum_flip.tile([P, CHUNK], F32, tag="flipped")
+                        columns_matmul(i - COLUMNS, sim_t)
                     if sums_due is not None:
                         batch_sums(sums_due)
                     if is_f0_chunk(i - MCONF):
@@ -484,11 +469,11 @@ def tile_coarsematching_t_kernel(tc, feat_c0, feat_c1, W, b, h0c, w0c, h1c, w1c,
                     if is_f0_chunk(i - ROWS):
                         column_maxima_chunk(i - ROWS)
                         rows_exp(i - ROWS)
+                    if last_of_batch(i - ROWS) is not None:
+                        column_maxima(last_of_batch(i - ROWS))
                     if sums_due is not None:
                         goal1_copy(sums_due)
                     if is_f0_chunk(i - BACK):
                         back_copy(i - BACK, conf1_bank)
                     if is_f0_chunk(i - FINISH_ROWS):
                         row_signs(i - FINISH_ROWS)
-                    if last_of_batch(i - ROWS) is not None:
-                        column_maxima_part(last_of_batch(i - ROWS))

@@ -31,8 +31,9 @@ ROWS = 1
 FINISH_ROWS = 2
 COLUMNS = 4
 BACK = 7
-GAPS = 8
-MCONF = 9
+BAR = 6
+KEPT = 7
+MCONF = 8
 LEAD = 2
 
 FLOPS = 2 * (8 * 1536 + 8 * 128) * 512 * 512 + 2 * 8 * 1536 * 128 * 512
@@ -50,6 +51,7 @@ def tile_coarsematching_t_kernel(tc, feat_c0, feat_c1, W, b, h0c, w0c, h1c, w1c,
     in_rows = h1c - 2 * BORDER
     in_cols = w1c - 2 * BORDER
     shape = [P, TILES, in_rows, in_cols]
+    batch_shape = [P, per_part, in_rows, in_cols]
 
     with ExitStack() as ctx:
         keep = ctx.enter_context(tc.tile_pool(name="keep", bufs=1))
@@ -57,7 +59,7 @@ def tile_coarsematching_t_kernel(tc, feat_c0, feat_c1, W, b, h0c, w0c, h1c, w1c,
         stage = ctx.enter_context(tc.tile_pool(name="stage", bufs=3))
         to_columns = ctx.enter_context(tc.tile_pool(name="to_columns", bufs=COLUMNS - ROWS + 2))
         to_back = ctx.enter_context(tc.tile_pool(name="to_back", bufs=BACK - COLUMNS + 2))
-        to_mconf = ctx.enter_context(tc.tile_pool(name="to_mconf", bufs=MCONF - ROWS + 2))
+        to_mconf = ctx.enter_context(tc.tile_pool(name="to_mconf", bufs=BACK - ROWS + 2))
         late = ctx.enter_context(tc.tile_pool(name="late", bufs=3))
         by_batch = ctx.enter_context(tc.tile_pool(name="by_batch", bufs=(BACK - ROWS) // banks + 3))
         psum_flip = ctx.enter_context(tc.psum_pool(name="psum_flip", bufs=2))
@@ -94,8 +96,8 @@ def tile_coarsematching_t_kernel(tc, feat_c0, feat_c1, W, b, h0c, w0c, h1c, w1c,
         nc.vector.tensor_scalar(out=sink[:], in0=inside[:], scalar1=1.0, scalar2=FAR, op0=ALU.subtract, op1=ALU.mult)
 
         mconf_tiles = []
-        for c in range(2 * banks):
-            mconf_tile = keep.tile([P, TILES, P], F32, name="mconf%d" % c)
+        for c in range(3):
+            mconf_tile = keep.tile([P, per_part, P], F32, name="mconf%d" % c)
             nc.vector.memset(mconf_tile[:], 0.0)
             mconf_tiles.append(mconf_tile)
 
@@ -200,7 +202,7 @@ def tile_coarsematching_t_kernel(tc, feat_c0, feat_c1, W, b, h0c, w0c, h1c, w1c,
                 out=codes.bitcast(FP8X4), scales=scales, in_=f_grouped[i][:].rearrange("p a r t -> p (a r t)")
             )
 
-        sim, conf0, sim_in, miss, conf1_t, conf1 = {}, {}, {}, {}, {}, {}
+        sim, conf0, sim_in, bar, conf1_t, larger = {}, {}, {}, {}, {}, {}
         row_max, row_sum, recip0 = {}, {}, {}
         sim_t_early, col_max_chunks, col_max, shift1, col_sum = {}, {}, {}, {}, {}
         recip1_diag, goal1_rep, goal1_bank, goal1_all = {}, {}, {}, {}
@@ -227,8 +229,12 @@ def tile_coarsematching_t_kernel(tc, feat_c0, feat_c1, W, b, h0c, w0c, h1c, w1c,
                 )
 
         def row_maxima(i):
-            row_max[i] = late.tile([P, TILES], F32, tag="row_max", name="row_max")
-            nc.vector.tensor_reduce(out=row_max[i][:], in_=sim[i][:], axis=AXIS.X, op=ALU.max)
+            n, c = batch_and_bank(i)
+            if c == 0:
+                row_max[n] = by_batch.tile([P, per_part], F32, tag="row_max", name="row_max")
+                recip0[n] = by_batch.tile([P, per_part], F32, tag="recip0", name="recip0")
+                sim_in[n] = by_batch.tile(batch_shape, F32, tag="sim_in", name="sim_in")
+            nc.vector.tensor_reduce(out=row_max[n][:, c * TILES : (c + 1) * TILES], in_=sim[i][:], axis=AXIS.X, op=ALU.max)
 
         def column_maxima_chunk(i):
             n, c = batch_and_bank(i)
@@ -241,8 +247,7 @@ def tile_coarsematching_t_kernel(tc, feat_c0, feat_c1, W, b, h0c, w0c, h1c, w1c,
             shift0 = late.tile([P, TILES], F32, tag="shift0")
             row_sum[i] = late.tile([P, TILES], F32, tag="row_sum", name="row_sum")
             conf0[i] = to_mconf.tile([P, TILES, P], F32, tag="conf0", name="conf0")
-            sim_in[i] = to_mconf.tile(shape, F32, tag="sim_in", name="sim_in", bufs=GAPS - ROWS + 2)
-            nc.scalar.mul(out=shift0[:], in_=row_max[i][:], mul=-inv_temp)
+            nc.scalar.mul(out=shift0[:], in_=row_max[n][:, c * TILES : (c + 1) * TILES], mul=-inv_temp)
             for a in range(TILES):
                 nc.scalar.activation(
                     out=conf0[i][:, a, :],
@@ -255,7 +260,7 @@ def tile_coarsematching_t_kernel(tc, feat_c0, feat_c1, W, b, h0c, w0c, h1c, w1c,
             for a in range(0, TILES, 2):
                 j = c * TILES + a
                 nc.scalar.activation(
-                    out=sim_in[i][:, a : a + 2],
+                    out=sim_in[n][:, j : j + 2],
                     in_=interior(sim[i][:])[:, a : a + 2],
                     func=ACT.Identity,
                     bias=sink[:, j : j + 1],
@@ -272,28 +277,17 @@ def tile_coarsematching_t_kernel(tc, feat_c0, feat_c1, W, b, h0c, w0c, h1c, w1c,
             col_sum[n] = by_batch.tile([P, banks], F32, tag="col_sum", name="col_sum")
 
         def finish_conf0(i):
+            n, c = batch_and_bank(i)
             for a in range(TILES):
+                j = c * TILES + a
                 nc.scalar.activation(
-                    out=conf0[i][:, a, :], in_=conf0[i][:, a, :], func=ACT.Copy, scale=recip0[i][:, a : a + 1]
+                    out=conf0[i][:, a, :], in_=conf0[i][:, a, :], func=ACT.Copy, scale=recip0[n][:, j : j + 1]
                 )
             nc.sync.dma_start(out=out_chunk(0, i), in_=conf0[i][:])
 
-        def row_goals(i):
-            recip0[i] = late.tile([P, TILES], F32, tag="recip0", name="recip0")
-            nc.vector.reciprocal(out=recip0[i][:], in_=row_sum[i][:])
-            goal0 = late.tile([P, TILES], F32, tag="goal0")
-            nc.gpsimd.tensor_scalar(out=goal0[:], in0=recip0[i][:], scalar1=THR, scalar2=FAR, op0=ALU.is_le, op1=ALU.mult)
-            nc.gpsimd.tensor_tensor(out=goal0[:], in0=goal0[:], in1=row_max[i][:], op=ALU.add)
-            miss[i] = to_mconf.tile(shape, F32, tag="miss", name="miss")
-            nc.gpsimd.tensor_tensor(
-                out=miss[i][:],
-                in0=sim_in[i][:],
-                in1=goal0[:].unsqueeze(2).unsqueeze(3).to_broadcast(shape),
-                op=ALU.subtract,
-            )
-
-        def row_signs(i):
-            nc.scalar.activation(out=miss[i][:], in_=miss[i][:], func=ACT.Sign)
+        def row_recips(i):
+            n, c = batch_and_bank(i)
+            nc.vector.reciprocal(out=recip0[n][:, c * TILES : (c + 1) * TILES], in_=row_sum[i][:])
 
         def columns_matmul(i, sim_t):
             n = batch_and_bank(i)[0]
@@ -354,32 +348,40 @@ def tile_coarsematching_t_kernel(tc, feat_c0, feat_c1, W, b, h0c, w0c, h1c, w1c,
             return conf1_bank
 
         def back_copy(i, conf1_bank):
-            conf1[i] = late.tile([P, TILES, P], F32, tag="conf1", name="conf1", bufs=MCONF - BACK + 2)
-            nc.scalar.copy(out=conf1[i][:], in_=conf1_bank[:])
-            nc.sync.dma_start(out=out_chunk(1, i), in_=conf1[i][:])
+            conf1 = late.tile([P, TILES, P], F32, tag="conf1")
+            nc.scalar.copy(out=conf1[:], in_=conf1_bank[:])
+            nc.sync.dma_start(out=out_chunk(1, i), in_=conf1[:])
 
-        def gaps(i):
-            n = batch_and_bank(i)[0]
-            gap1 = late.tile(shape, F32, tag="gap1")
-            nc.gpsimd.tensor_tensor(
-                out=gap1[:], in0=sim_in[i][:], in1=interior(goal1_all[n][:]).to_broadcast(shape), op=ALU.subtract
+        def larger_chunk(i, conf1_bank):
+            n, c = batch_and_bank(i)
+            if c == 0:
+                larger[n] = by_batch.tile(batch_shape, F32, tag="larger", name="larger")
+            nc.vector.tensor_tensor(
+                out=larger[n][:, c * TILES : (c + 1) * TILES],
+                in0=interior(conf1_bank[:]),
+                in1=interior(conf0[i][:]),
+                op=ALU.max,
             )
-            nc.gpsimd.tensor_tensor(out=miss[i][:], in0=miss[i][:], in1=gap1[:], op=ALU.mult)
 
-        def mconf_chunk(i):
-            larger = late.tile(shape, F32, tag="larger")
-            nc.vector.tensor_tensor(out=larger[:], in0=interior(conf0[i][:]), in1=interior(conf1[i][:]), op=ALU.max)
-            mconf = mconf_tiles[i % len(mconf_tiles)]
-            for a in range(TILES):
-                nc.vector.scalar_tensor_tensor(
-                    out=interior(mconf[:])[:, a],
-                    in0=miss[i][:, a],
-                    scalar=0.0,
-                    in1=larger[:, a],
-                    op0=ALU.is_equal,
-                    op1=ALU.mult,
-                )
-            nc.sync.dma_start(out=out_chunk(2, i), in_=mconf[:])
+        def batch_bar(n):
+            goal0 = late.tile([P, per_part], F32, tag="goal0")
+            nc.vector.tensor_scalar(out=goal0[:], in0=recip0[n][:], scalar1=THR, scalar2=FAR, op0=ALU.is_le, op1=ALU.mult)
+            nc.vector.tensor_tensor(out=goal0[:], in0=goal0[:], in1=row_max[n][:], op=ALU.add)
+            bar[n] = by_batch.tile(batch_shape, F32, tag="bar", name="bar")
+            nc.vector.tensor_tensor(
+                out=bar[n][:],
+                in0=goal0[:].unsqueeze(2).unsqueeze(3).to_broadcast(batch_shape),
+                in1=interior(goal1_all[n][:]).to_broadcast(batch_shape),
+                op=ALU.min,
+            )
+
+        def batch_kept(n):
+            nc.vector.tensor_tensor(out=bar[n][:], in0=sim_in[n][:], in1=bar[n][:], op=ALU.is_ge)
+
+        def batch_mconf(n):
+            mconf = mconf_tiles[n % len(mconf_tiles)]
+            nc.vector.tensor_tensor(out=interior(mconf[:]), in0=bar[n][:], in1=larger[n][:], op=ALU.mult)
+            nc.sync.dma_start(out=out[2, n].rearrange("(p j) s -> p j s", j=per_part), in_=mconf[:])
 
         w_rows = keep.tile([P, PACK * FEAT], BF16)
         nc.sync.dma_start(out=w_rows[:], in_=W.rearrange("(p t) k -> p (t k)", t=PACK))
@@ -448,12 +450,14 @@ def tile_coarsematching_t_kernel(tc, feat_c0, feat_c1, W, b, h0c, w0c, h1c, w1c,
                         columns_matmul(i - COLUMNS, sim_t)
                     if sums_due is not None:
                         batch_sums(sums_due)
-                    if is_f0_chunk(i - MCONF):
-                        mconf_chunk(i - MCONF)
+                    if last_of_batch(i - MCONF) is not None:
+                        batch_mconf(last_of_batch(i - MCONF))
                     if is_f0_chunk(i - FINISH_ROWS):
-                        row_goals(i - FINISH_ROWS)
-                    if is_f0_chunk(i - GAPS):
-                        gaps(i - GAPS)
+                        row_recips(i - FINISH_ROWS)
+                    if last_of_batch(i - BAR) is not None:
+                        batch_bar(last_of_batch(i - BAR))
+                    if last_of_batch(i - KEPT) is not None:
+                        batch_kept(last_of_batch(i - KEPT))
                 if slot == 2:
                     if is_f0_chunk(i - ROWS):
                         row_maxima(i - ROWS)
@@ -475,5 +479,4 @@ def tile_coarsematching_t_kernel(tc, feat_c0, feat_c1, W, b, h0c, w0c, h1c, w1c,
                         goal1_copy(sums_due)
                     if is_f0_chunk(i - BACK):
                         back_copy(i - BACK, conf1_bank)
-                    if is_f0_chunk(i - FINISH_ROWS):
-                        row_signs(i - FINISH_ROWS)
+                        larger_chunk(i - BACK, conf1_bank)

@@ -35,6 +35,7 @@ BAR = 6
 KEPT = 7
 MCONF = 8
 LEAD = 2
+BY_SCALAR = (1,)
 
 FLOPS = 2 * (8 * 1536 + 8 * 128) * 512 * 512 + 2 * 8 * 1536 * 128 * 512
 
@@ -109,7 +110,7 @@ def tile_coarsematching_t_kernel(tc, feat_c0, feat_c1, W, b, h0c, w0c, h1c, w1c,
         n_chunks = f1_chunks + batches * banks
         chunk_elems = TILES * FEAT
         f0_rows = {}
-        x_grouped, x_codes, x_scales, f_grouped, f0_codes, f0_scales = {}, {}, {}, {}, {}, {}
+        x_grouped, x_codes, x_scales, f_grouped, f0_codes, f0_scales, f_planes = {}, {}, {}, {}, {}, {}, {}
         acc = {}
 
         def is_chunk(i):
@@ -120,6 +121,9 @@ def tile_coarsematching_t_kernel(tc, feat_c0, feat_c1, W, b, h0c, w0c, h1c, w1c,
 
         def batch_and_bank(i):
             return divmod(i - f1_chunks, banks)
+
+        def by_scalar(i):
+            return is_f0_chunk(i) and batch_and_bank(i)[1] in BY_SCALAR
 
         def flip_rows(rows, bank_pool, bank_tag):
             words = rows.bitcast(F32)
@@ -163,6 +167,19 @@ def tile_coarsematching_t_kernel(tc, feat_c0, feat_c1, W, b, h0c, w0c, h1c, w1c,
 
         def project_tile(g):
             i, a = divmod(g, TILES)
+            if by_scalar(i):
+                acc[g] = psum_proj.tile([P, CHUNK], F32, tag="acc", name="acc")
+                w_cols = slice(a * P, (a + 1) * P)
+                nc.tensor.matmul_mx(
+                    out=acc[g][:],
+                    lhsT=w_codes[:, w_cols].bitcast(FP8X4),
+                    lhsT_scale=w_scales[:, w_cols],
+                    rhs=x_codes[i][:].bitcast(FP8X4),
+                    rhs_scale=x_scales[i][:],
+                    start=True,
+                    stop=True,
+                )
+                return
             acc[g] = psum_proj.tile([P, PACK, P], F32, tag="acc", name="acc")
             x_cols = slice(a * P, (a + 1) * P)
             for t in range(PACK):
@@ -179,6 +196,13 @@ def tile_coarsematching_t_kernel(tc, feat_c0, feat_c1, W, b, h0c, w0c, h1c, w1c,
 
         def empty_tile(g):
             i, a = divmod(g, TILES)
+            if by_scalar(i):
+                if a == 0:
+                    f_planes[i] = stage.tile([P, PACK, CHUNK], BF16, tag="f_planes", name="f_planes")
+                nc.scalar.activation(
+                    out=f_planes[i][:, a, :], in_=acc[g][:], func=ACT.Identity, bias=bias[:, a : a + 1], scale=inv_scale
+                )
+                return
             if a == 0:
                 f_grouped[i] = stage.tile([P, TILES, P, PACK], BF16, tag="f_grouped", name="f_grouped", align_bytes=64)
             nc.vector.scalar_tensor_tensor(
@@ -188,6 +212,12 @@ def tile_coarsematching_t_kernel(tc, feat_c0, feat_c1, W, b, h0c, w0c, h1c, w1c,
                 in1=bias_by_row,
                 op0=ALU.mult,
                 op1=ALU.add,
+            )
+
+        def interleave_f(i):
+            f_grouped[i] = stage.tile([P, TILES, P, PACK], BF16, tag="f_grouped", name="f_grouped", align_bytes=64)
+            nc.vector.tensor_copy(
+                out=f_grouped[i][:].rearrange("p a r t -> p (a r) t"), in_=f_planes[i][:].rearrange("p t r -> p r t")
             )
 
         def quantise_f(i):
@@ -429,6 +459,8 @@ def tile_coarsematching_t_kernel(tc, feat_c0, feat_c1, W, b, h0c, w0c, h1c, w1c,
                 g = i * TILES + slot
                 if is_chunk((g + LEAD) // TILES):
                     project_tile(g + LEAD)
+                if slot == 0 and by_scalar(i - ROWS):
+                    interleave_f(i - ROWS)
                 if is_chunk(i - PROJECT):
                     empty_tile(g)
                 if slot == 0:

@@ -233,7 +233,7 @@ def tile_coarsematching_t_kernel(tc, feat_c0, feat_c1, W, b, h0c, w0c, h1c, w1c,
             )
 
         sim, conf0, sim_in, bar, conf1_t, larger = {}, {}, {}, {}, {}, {}
-        row_max, row_sum, recip0 = {}, {}, {}
+        row_max, row_sum, recip0, shift0, recip1, goal1, goal0 = {}, {}, {}, {}, {}, {}, {}
         sim_t_early, col_max_chunks, col_max, shift1, col_sum = {}, {}, {}, {}, {}
         recip1_diag, goal1_rep, goal1_bank, goal1_all = {}, {}, {}, {}
         inv_temp = 1.0 / TEMPERATURE
@@ -272,18 +272,21 @@ def tile_coarsematching_t_kernel(tc, feat_c0, feat_c1, W, b, h0c, w0c, h1c, w1c,
                 col_max_chunks[n] = by_batch.tile([P, banks], F32, tag="col_max_chunks", name="col_max_chunks")
             nc.vector.tensor_reduce(out=col_max_chunks[n][:, c : c + 1], in_=sim_t_early[i][:], axis=AXIS.X, op=ALU.max)
 
+        def rows_shift(i):
+            n, c = batch_and_bank(i)
+            shift0[i] = late.tile([P, TILES], F32, tag="shift0", name="shift0")
+            nc.scalar.mul(out=shift0[i][:], in_=row_max[n][:, c * TILES : (c + 1) * TILES], mul=-inv_temp)
+
         def rows_exp(i):
             n, c = batch_and_bank(i)
-            shift0 = late.tile([P, TILES], F32, tag="shift0")
             row_sum[i] = late.tile([P, TILES], F32, tag="row_sum", name="row_sum")
             conf0[i] = to_mconf.tile([P, TILES, P], F32, tag="conf0", name="conf0")
-            nc.scalar.mul(out=shift0[:], in_=row_max[n][:, c * TILES : (c + 1) * TILES], mul=-inv_temp)
             for a in range(TILES):
                 nc.scalar.activation(
                     out=conf0[i][:, a, :],
                     in_=sim[i][:, a, :],
                     func=ACT.Exp,
-                    bias=shift0[:, a : a + 1],
+                    bias=shift0[i][:, a : a + 1],
                     scale=inv_temp,
                     accum_out=row_sum[i][:, a : a + 1],
                 )
@@ -344,17 +347,29 @@ def tile_coarsematching_t_kernel(tc, feat_c0, feat_c1, W, b, h0c, w0c, h1c, w1c,
                 accum_out=col_sum[n][:, c : c + 1],
             )
 
-        def batch_sums(n):
-            recip1 = late.tile([P, 1], F32, tag="recip1")
-            nc.vector.tensor_reduce(out=recip1[:], in_=col_sum[n][:], axis=AXIS.X, op=ALU.add)
-            nc.vector.reciprocal(out=recip1[:], in_=recip1[:])
+        def sums_add(n):
+            recip1[n] = late.tile([P, 1], F32, tag="recip1", name="recip1")
+            nc.vector.tensor_reduce(out=recip1[n][:], in_=col_sum[n][:], axis=AXIS.X, op=ALU.add)
+
+        def sums_recip(n):
+            nc.vector.reciprocal(out=recip1[n][:], in_=recip1[n][:])
+
+        def sums_diag(n):
             recip1_diag[n] = by_batch.tile([P, P], F32, tag="recip1_diag", name="recip1_diag")
-            nc.vector.tensor_scalar_mul(out=recip1_diag[n][:], in0=ident[:], scalar1=recip1[:])
-            goal1 = late.tile([P, 1], F32, tag="goal1")
-            nc.vector.tensor_scalar(out=goal1[:], in0=recip1[:], scalar1=THR, scalar2=FAR, op0=ALU.is_le, op1=ALU.mult)
-            nc.vector.tensor_tensor(out=goal1[:], in0=goal1[:], in1=col_max[n][:], op=ALU.add)
+            nc.vector.tensor_scalar_mul(out=recip1_diag[n][:], in0=ident[:], scalar1=recip1[n][:])
+
+        def goal1_far(n):
+            goal1[n] = late.tile([P, 1], F32, tag="goal1", name="goal1")
+            nc.vector.tensor_scalar(
+                out=goal1[n][:], in0=recip1[n][:], scalar1=THR, scalar2=FAR, op0=ALU.is_le, op1=ALU.mult
+            )
+
+        def goal1_add(n):
+            nc.vector.tensor_tensor(out=goal1[n][:], in0=goal1[n][:], in1=col_max[n][:], op=ALU.add)
+
+        def goal1_spread(n):
             goal1_rep[n] = late.tile([P, P], F32, tag="goal1_rep", name="goal1_rep")
-            nc.vector.tensor_copy(out=goal1_rep[n][:], in_=goal1[:].to_broadcast([P, P]))
+            nc.vector.tensor_copy(out=goal1_rep[n][:], in_=goal1[n][:].to_broadcast([P, P]))
 
         def goal1_flip(n):
             goal1_bank[n] = psum_flip.tile([P, P], F32, tag="flipped", name="goal1_bank")
@@ -393,14 +408,20 @@ def tile_coarsematching_t_kernel(tc, feat_c0, feat_c1, W, b, h0c, w0c, h1c, w1c,
                 op=ALU.max,
             )
 
+        def goal0_far(n):
+            goal0[n] = late.tile([P, per_part], F32, tag="goal0", name="goal0")
+            nc.vector.tensor_scalar(
+                out=goal0[n][:], in0=recip0[n][:], scalar1=THR, scalar2=FAR, op0=ALU.is_le, op1=ALU.mult
+            )
+
+        def goal0_add(n):
+            nc.vector.tensor_tensor(out=goal0[n][:], in0=goal0[n][:], in1=row_max[n][:], op=ALU.add)
+
         def batch_bar(n):
-            goal0 = late.tile([P, per_part], F32, tag="goal0")
-            nc.vector.tensor_scalar(out=goal0[:], in0=recip0[n][:], scalar1=THR, scalar2=FAR, op0=ALU.is_le, op1=ALU.mult)
-            nc.vector.tensor_tensor(out=goal0[:], in0=goal0[:], in1=row_max[n][:], op=ALU.add)
             bar[n] = by_batch.tile(batch_shape, F32, tag="bar", name="bar")
             nc.vector.tensor_tensor(
                 out=bar[n][:],
-                in0=goal0[:].unsqueeze(2).unsqueeze(3).to_broadcast(batch_shape),
+                in0=goal0[n][:].unsqueeze(2).unsqueeze(3).to_broadcast(batch_shape),
                 in1=interior(goal1_all[n][:]).to_broadcast(batch_shape),
                 op=ALU.min,
             )
@@ -455,6 +476,9 @@ def tile_coarsematching_t_kernel(tc, feat_c0, feat_c1, W, b, h0c, w0c, h1c, w1c,
                 load_batch(n + 2)
             maxima_due = last_of_batch(i - ROWS - 1)
             sums_due = last_of_batch(i - COLUMNS - 1)
+            bar_due = last_of_batch(i - BAR)
+            kept_due = last_of_batch(i - KEPT)
+            mconf_due = last_of_batch(i - MCONF)
             for slot in range(TILES):
                 g = i * TILES + slot
                 if is_chunk((g + LEAD) // TILES):
@@ -466,10 +490,16 @@ def tile_coarsematching_t_kernel(tc, feat_c0, feat_c1, W, b, h0c, w0c, h1c, w1c,
                 if slot == 0:
                     if is_chunk(i - ROWS):
                         quantise_f(i - ROWS)
+                    if sums_due is not None:
+                        sums_add(sums_due)
                     if is_chunk(i - QUANTISE_X):
                         quantise_x(i - QUANTISE_X)
+                    if sums_due is not None:
+                        sums_recip(sums_due)
                     if is_chunk(i - FLIP):
                         flip(i - FLIP)
+                    if bar_due is not None:
+                        goal0_far(bar_due)
                 if slot == 1:
                     if is_f0_chunk(i - ROWS):
                         rows_matmul(i - ROWS)
@@ -480,23 +510,28 @@ def tile_coarsematching_t_kernel(tc, feat_c0, feat_c1, W, b, h0c, w0c, h1c, w1c,
                     if is_f0_chunk(i - COLUMNS):
                         sim_t = psum_flip.tile([P, CHUNK], F32, tag="flipped")
                         columns_matmul(i - COLUMNS, sim_t)
-                    if sums_due is not None:
-                        batch_sums(sums_due)
-                    if last_of_batch(i - MCONF) is not None:
-                        batch_mconf(last_of_batch(i - MCONF))
                     if is_f0_chunk(i - FINISH_ROWS):
                         row_recips(i - FINISH_ROWS)
-                    if last_of_batch(i - BAR) is not None:
-                        batch_bar(last_of_batch(i - BAR))
-                    if last_of_batch(i - KEPT) is not None:
-                        batch_kept(last_of_batch(i - KEPT))
+                    if sums_due is not None:
+                        sums_diag(sums_due)
+                        goal1_far(sums_due)
+                    if mconf_due is not None:
+                        batch_mconf(mconf_due)
+                    if bar_due is not None:
+                        goal0_add(bar_due)
+                    if kept_due is not None:
+                        batch_kept(kept_due)
+                    if sums_due is not None:
+                        goal1_add(sums_due)
                 if slot == 2:
                     if is_f0_chunk(i - ROWS):
                         row_maxima(i - ROWS)
-                    if is_f0_chunk(i - COLUMNS):
-                        columns_exp(i - COLUMNS, sim_t)
+                    if sums_due is not None:
+                        goal1_spread(sums_due)
                     if is_f0_chunk(i - FINISH_ROWS):
                         finish_conf0(i - FINISH_ROWS)
+                    if is_f0_chunk(i - COLUMNS):
+                        columns_exp(i - COLUMNS, sim_t)
                     if sums_due is not None:
                         goal1_flip(sums_due)
                     if is_f0_chunk(i - BACK):
@@ -504,11 +539,15 @@ def tile_coarsematching_t_kernel(tc, feat_c0, feat_c1, W, b, h0c, w0c, h1c, w1c,
                 if slot == 3:
                     if is_f0_chunk(i - ROWS):
                         column_maxima_chunk(i - ROWS)
+                        rows_shift(i - ROWS)
+                    if is_f0_chunk(i - BACK):
+                        back_copy(i - BACK, conf1_bank)
+                        larger_chunk(i - BACK, conf1_bank)
+                    if is_f0_chunk(i - ROWS):
                         rows_exp(i - ROWS)
+                    if bar_due is not None:
+                        batch_bar(bar_due)
                     if last_of_batch(i - ROWS) is not None:
                         column_maxima(last_of_batch(i - ROWS))
                     if sums_due is not None:
                         goal1_copy(sums_due)
-                    if is_f0_chunk(i - BACK):
-                        back_copy(i - BACK, conf1_bank)
-                        larger_chunk(i - BACK, conf1_bank)

@@ -33,9 +33,9 @@ COLUMNS = 4
 BACK = 7
 BAR = 6
 KEPT = 7
-MCONF = 8
+MCONF = 7
 LEAD = 2
-BY_SCALAR = (1,)
+BY_SCALAR = 2
 
 FLOPS = 2 * (8 * 1536 + 8 * 128) * 512 * 512 + 2 * 8 * 1536 * 128 * 512
 
@@ -123,7 +123,7 @@ def tile_coarsematching_t_kernel(tc, feat_c0, feat_c1, W, b, h0c, w0c, h1c, w1c,
             return divmod(i - f1_chunks, banks)
 
         def by_scalar(i):
-            return is_f0_chunk(i) and batch_and_bank(i)[1] in BY_SCALAR
+            return is_f0_chunk(i) and (i - f1_chunks) % BY_SCALAR == 1
 
         def flip_rows(rows, bank_pool, bank_tag):
             words = rows.bitcast(F32)
@@ -143,7 +143,10 @@ def tile_coarsematching_t_kernel(tc, feat_c0, feat_c1, W, b, h0c, w0c, h1c, w1c,
 
         def load_batch(n):
             f0_rows[n] = rows_pool.tile([P, per_part * FEAT], BF16, tag="rows", name="f0_rows")
-            nc.sync.dma_start(out=f0_rows[n][:], in_=feat_c0[n].rearrange("(p j) k -> p (j k)", j=per_part))
+            rows_in = feat_c0[n].rearrange("(p j) k -> p (j k)", j=per_part)
+            for c in range(banks):
+                cols = slice(c * chunk_elems, (c + 1) * chunk_elems)
+                nc.sync.dma_start(out=f0_rows[n][:, cols], in_=rows_in[:, cols])
 
         def flip(i):
             if i < f1_chunks:
@@ -429,10 +432,14 @@ def tile_coarsematching_t_kernel(tc, feat_c0, feat_c1, W, b, h0c, w0c, h1c, w1c,
         def batch_kept(n):
             nc.vector.tensor_tensor(out=bar[n][:], in0=sim_in[n][:], in1=bar[n][:], op=ALU.is_ge)
 
-        def batch_mconf(n):
+        def batch_mconf(n, first, last):
             mconf = mconf_tiles[n % len(mconf_tiles)]
-            nc.vector.tensor_tensor(out=interior(mconf[:]), in0=bar[n][:], in1=larger[n][:], op=ALU.mult)
-            nc.sync.dma_start(out=out[2, n].rearrange("(p j) s -> p j s", j=per_part), in_=mconf[:])
+            nc.vector.tensor_tensor(
+                out=interior(mconf[:])[:, first:last], in0=bar[n][:, first:last], in1=larger[n][:, first:last], op=ALU.mult
+            )
+            nc.sync.dma_start(
+                out=out[2, n].rearrange("(p j) s -> p j s", j=per_part)[:, first:last, :], in_=mconf[:, first:last, :]
+            )
 
         w_rows = keep.tile([P, PACK * FEAT], BF16)
         nc.sync.dma_start(out=w_rows[:], in_=W.rearrange("(p t) k -> p (t k)", t=PACK))
@@ -481,12 +488,22 @@ def tile_coarsematching_t_kernel(tc, feat_c0, feat_c1, W, b, h0c, w0c, h1c, w1c,
             mconf_due = last_of_batch(i - MCONF)
             for slot in range(TILES):
                 g = i * TILES + slot
-                if is_chunk((g + LEAD) // TILES):
-                    project_tile(g + LEAD)
-                if slot == 0 and by_scalar(i - ROWS):
-                    interleave_f(i - ROWS)
-                if is_chunk(i - PROJECT):
-                    empty_tile(g)
+                if by_scalar(i):
+                    if slot == 0:
+                        project_tile(g + LEAD)
+                        project_tile(g + LEAD + 1)
+                    if slot < 2:
+                        empty_tile(i * TILES + 2 * slot)
+                        empty_tile(i * TILES + 2 * slot + 1)
+                    if slot >= 2 and is_chunk(i + 1):
+                        project_tile(g + LEAD)
+                    if slot == 3:
+                        interleave_f(i)
+                else:
+                    if is_chunk((g + LEAD) // TILES):
+                        project_tile(g + LEAD)
+                    if is_chunk(i - PROJECT):
+                        empty_tile(g)
                 if slot == 0:
                     if is_chunk(i - ROWS):
                         quantise_f(i - ROWS)
@@ -515,14 +532,14 @@ def tile_coarsematching_t_kernel(tc, feat_c0, feat_c1, W, b, h0c, w0c, h1c, w1c,
                     if sums_due is not None:
                         sums_diag(sums_due)
                         goal1_far(sums_due)
-                    if mconf_due is not None:
-                        batch_mconf(mconf_due)
                     if bar_due is not None:
                         goal0_add(bar_due)
                     if kept_due is not None:
                         batch_kept(kept_due)
                     if sums_due is not None:
                         goal1_add(sums_due)
+                    if mconf_due is not None:
+                        batch_mconf(mconf_due, 0, per_part - TILES)
                 if slot == 2:
                     if is_f0_chunk(i - ROWS):
                         row_maxima(i - ROWS)
@@ -547,6 +564,8 @@ def tile_coarsematching_t_kernel(tc, feat_c0, feat_c1, W, b, h0c, w0c, h1c, w1c,
                         rows_exp(i - ROWS)
                     if bar_due is not None:
                         batch_bar(bar_due)
+                    if mconf_due is not None:
+                        batch_mconf(mconf_due, per_part - TILES, per_part)
                     if last_of_batch(i - ROWS) is not None:
                         column_maxima(last_of_batch(i - ROWS))
                     if sums_due is not None:

@@ -220,7 +220,8 @@ def tile_coarsematching_t_kernel(tc, feat_c0, feat_c1, W, b, h0c, w0c, h1c, w1c,
         def interleave_f(i):
             f_grouped[i] = stage.tile([P, TILES, P, PACK], BF16, tag="f_grouped", name="f_grouped", align_bytes=64)
             nc.vector.tensor_copy(
-                out=f_grouped[i][:].rearrange("p a r t -> p (a r) t"), in_=f_planes[i][:].rearrange("p t r -> p r t")
+                out=f_grouped[i][:].rearrange("p a (c e) t -> p (a c) t e", e=4),
+                in_=f_planes[i][:].rearrange("p t (c e) -> p c t e", e=4),
             )
 
         def quantise_f(i):

from contextlib import ExitStack

import concourse.mybir as mybir
from concourse.masks import make_identity

F32 = mybir.dt.float32
BF16 = mybir.dt.bfloat16
U32 = mybir.dt.uint32
U8 = mybir.dt.uint8
I32 = mybir.dt.int32
FP8X4 = mybir.dt.float8_e4m3fn_x4
ALU = mybir.AluOpType
ACT = mybir.ActivationFunctionType
AXIS = mybir.AxisListType

P = 128
PACK = 4
FEAT = P * PACK
TILES = 4
CHUNK = TILES * P

THR = 0.2
TEMPERATURE = 0.1
BORDER = 2
FAR = 1.0e30

FLIP = -2
QUANTISE_X = -1
PROJECT = 0
ROWS = 1
FINISH_ROWS = 2
COLUMNS = 4
BACK = 7
BAR = 6
KEPT = 7
MCONF = 7
LEAD = 2
BY_SCALAR = 2

FLOPS = 2 * (8 * 1536 + 8 * 128) * 512 * 512 + 2 * 8 * 1536 * 128 * 512


def tile_coarsematching_t_kernel(tc, feat_c0, feat_c1, W, b, h0c, w0c, h1c, w1c, out):
    nc = tc.nc
    batches, cells0, feat = feat_c0.shape
    cells1 = feat_c1.shape[1]
    per_part = cells0 // P
    banks = per_part // TILES
    parts_per_row = w0c // per_part
    assert feat == FEAT and cells1 == P and cells0 == h0c * w0c and cells1 == h1c * w1c
    assert per_part % TILES == 0 and batches % TILES == 0 and parts_per_row == 4 and BORDER == 2
    in_rows = h1c - 2 * BORDER
    in_cols = w1c - 2 * BORDER
    shape = [P, TILES, in_rows, in_cols]
    batch_shape = [P, per_part, in_rows, in_cols]

    with ExitStack() as ctx:
        keep = ctx.enter_context(tc.tile_pool(name="keep", bufs=1))
        rows_pool = ctx.enter_context(tc.tile_pool(name="rows", bufs=3))
        stage = ctx.enter_context(tc.tile_pool(name="stage", bufs=3))
        to_columns = ctx.enter_context(tc.tile_pool(name="to_columns", bufs=COLUMNS - ROWS + 2))
        to_back = ctx.enter_context(tc.tile_pool(name="to_back", bufs=BACK - COLUMNS + 2))
        to_mconf = ctx.enter_context(tc.tile_pool(name="to_mconf", bufs=BACK - ROWS + 2))
        late = ctx.enter_context(tc.tile_pool(name="late", bufs=3))
        by_batch = ctx.enter_context(tc.tile_pool(name="by_batch", bufs=(BACK - ROWS) // banks + 3))
        psum_flip = ctx.enter_context(tc.psum_pool(name="psum_flip", bufs=2))
        psum_proj = ctx.enter_context(tc.psum_pool(name="psum_proj", bufs=LEAD + 1))
        psum_match = ctx.enter_context(tc.psum_pool(name="psum_match", bufs=1))

        ident = keep.tile([P, P], F32)
        make_identity(nc, ident[:])

        part_i = keep.tile([P, per_part], I32)
        nc.gpsimd.iota(part_i[:], pattern=[[0, per_part]], base=0, channel_multiplier=1)
        j_i = keep.tile([P, per_part], I32)
        nc.gpsimd.iota(j_i[:], pattern=[[1, per_part]], base=0, channel_multiplier=0)
        sub_i = keep.tile([P, per_part], I32)
        nc.vector.tensor_single_scalar(out=sub_i[:], in_=part_i[:], scalar=parts_per_row - 1, op=ALU.bitwise_and)
        col = keep.tile([P, per_part], F32)
        nc.vector.scalar_tensor_tensor(
            out=col[:], in0=sub_i[:], scalar=float(per_part), in1=j_i[:], op0=ALU.mult, op1=ALU.add
        )
        inside = keep.tile([P, per_part], F32)
        nc.vector.tensor_single_scalar(out=inside[:], in_=col[:], scalar=float(BORDER), op=ALU.is_ge)
        nc.vector.scalar_tensor_tensor(
            out=inside[:], in0=col[:], scalar=float(w0c - BORDER), in1=inside[:], op0=ALU.is_lt, op1=ALU.mult
        )
        nc.vector.scalar_tensor_tensor(
            out=inside[:], in0=part_i[:], scalar=float(parts_per_row * BORDER), in1=inside[:],
            op0=ALU.is_ge, op1=ALU.mult,
        )
        nc.vector.scalar_tensor_tensor(
            out=inside[:], in0=part_i[:], scalar=float(parts_per_row * (h0c - BORDER)), in1=inside[:],
            op0=ALU.is_lt, op1=ALU.mult,
        )
        sink = keep.tile([P, per_part], F32)
        nc.vector.tensor_scalar(out=sink[:], in0=inside[:], scalar1=1.0, scalar2=FAR, op0=ALU.subtract, op1=ALU.mult)

        mconf_tiles = []
        for c in range(3):
            mconf_tile = keep.tile([P, per_part, P], F32, name="mconf%d" % c)
            nc.vector.memset(mconf_tile[:], 0.0)
            mconf_tiles.append(mconf_tile)

        def interior(plane):
            grid = plane.rearrange("p j (r c) -> p j r c", c=w1c)
            return grid[:, :, BORDER : h1c - BORDER, BORDER : w1c - BORDER]

        f1_chunks = batches // TILES
        n_chunks = f1_chunks + batches * banks
        chunk_elems = TILES * FEAT
        f0_rows = {}
        x_grouped, x_codes, x_scales, f_grouped, f0_codes, f0_scales, f_planes = {}, {}, {}, {}, {}, {}, {}
        acc = {}

        def is_chunk(i):
            return 0 <= i < n_chunks

        def is_f0_chunk(i):
            return f1_chunks <= i < n_chunks

        def batch_and_bank(i):
            return divmod(i - f1_chunks, banks)

        def by_scalar(i):
            return is_f0_chunk(i) and (i - f1_chunks) % BY_SCALAR == 1

        def flip_rows(rows, bank_pool, bank_tag):
            words = rows.bitcast(F32)
            grouped = stage.tile([P, CHUNK * PACK], BF16, tag="x_grouped", align_bytes=64)
            grouped_words = grouped[:].bitcast(F32).rearrange("q (a r u) -> q a r u", a=TILES, u=2)
            for pair in range(TILES // 2):
                flipped = bank_pool.tile([P, 2, 2, P], F32, tag=bank_tag, name="flipped")
                for a in range(2):
                    for u in range(2):
                        first = ((2 * pair + a) * 2 + u) * P
                        nc.tensor.transpose(flipped[:, a, u, :], words[:, first : first + P], ident[:])
                nc.scalar.copy(
                    out=grouped_words[:, 2 * pair : 2 * pair + 2],
                    in_=flipped[:].rearrange("q a u r -> q a r u"),
                )
            return grouped

        def load_batch(n):
            f0_rows[n] = rows_pool.tile([P, per_part * FEAT], BF16, tag="rows", name="f0_rows")
            rows_in = feat_c0[n].rearrange("(p j) k -> p (j k)", j=per_part)
            for c in range(banks):
                cols = slice(c * chunk_elems, (c + 1) * chunk_elems)
                nc.sync.dma_start(out=f0_rows[n][:, cols], in_=rows_in[:, cols])

        def flip(i):
            if i < f1_chunks:
                rows = f1_rows[:, i * chunk_elems : (i + 1) * chunk_elems]
            else:
                n, c = batch_and_bank(i)
                rows = f0_rows[n][:, c * chunk_elems : (c + 1) * chunk_elems]
            x_grouped[i] = flip_rows(rows, psum_flip, "flipped")

        def quantise_x(i, pieces=1):
            x_codes[i] = stage.tile([P, CHUNK], U32, tag="x_codes", name="x_codes", align_bytes=64)
            x_scales[i] = stage.tile([P, CHUNK], U8, tag="x_scales", name="x_scales", align_bytes=64)
            width = CHUNK // pieces
            for piece in range(pieces):
                cols = slice(piece * width, (piece + 1) * width)
                nc.vector.quantize_mx(
                    out=x_codes[i][:, cols].bitcast(FP8X4),
                    scales=x_scales[i][:, cols],
                    in_=x_grouped[i][:, piece * width * PACK : (piece + 1) * width * PACK],
                )

        def project_tile(g):
            i, a = divmod(g, TILES)
            if by_scalar(i):
                acc[g] = psum_proj.tile([P, CHUNK], F32, tag="acc", name="acc")
                w_cols = slice(a * P, (a + 1) * P)
                nc.tensor.matmul_mx(
                    out=acc[g][:],
                    lhsT=w_codes[:, w_cols].bitcast(FP8X4),
                    lhsT_scale=w_scales[:, w_cols],
                    rhs=x_codes[i][:].bitcast(FP8X4),
                    rhs_scale=x_scales[i][:],
                    start=True,
                    stop=True,
                )
                return
            acc[g] = psum_proj.tile([P, PACK, P], F32, tag="acc", name="acc")
            x_cols = slice(a * P, (a + 1) * P)
            for t in range(PACK):
                w_cols = slice(t * P, (t + 1) * P)
                nc.tensor.matmul_mx(
                    out=acc[g][:, t, :],
                    lhsT=w_codes[:, w_cols].bitcast(FP8X4),
                    lhsT_scale=w_scales[:, w_cols],
                    rhs=x_codes[i][:, x_cols].bitcast(FP8X4),
                    rhs_scale=x_scales[i][:, x_cols],
                    start=True,
                    stop=True,
                )

        def empty_tile(g):
            i, a = divmod(g, TILES)
            if by_scalar(i):
                if a == 0:
                    f_planes[i] = stage.tile([P, PACK, CHUNK], BF16, tag="f_planes", name="f_planes")
                nc.scalar.activation(
                    out=f_planes[i][:, a, :], in_=acc[g][:], func=ACT.Identity, bias=bias[:, a : a + 1], scale=inv_scale
                )
                return
            if a == 0:
                f_grouped[i] = stage.tile([P, TILES, P, PACK], BF16, tag="f_grouped", name="f_grouped", align_bytes=64)
            nc.vector.scalar_tensor_tensor(
                out=f_grouped[i][:, a],
                in0=acc[g][:].rearrange("p t r -> p r t"),
                scalar=inv_scale,
                in1=bias_by_row,
                op0=ALU.mult,
                op1=ALU.add,
            )

        def interleave_f(i):
            f_grouped[i] = stage.tile([P, TILES, P, PACK], BF16, tag="f_grouped", name="f_grouped", align_bytes=64)
            nc.vector.tensor_copy(
                out=f_grouped[i][:].rearrange("p a (c e) t -> p (a c) t e", e=4),
                in_=f_planes[i][:].rearrange("p t (c e) -> p c t e", e=4),
            )

        def quantise_f(i):
            if i < f1_chunks:
                cols = slice(i * CHUNK, (i + 1) * CHUNK)
                codes, scales = f1_codes[:, cols], f1_scales[:, cols]
            else:
                f0_codes[i] = to_columns.tile([P, CHUNK], U32, tag="f0_codes", name="f0_codes", align_bytes=64)
                f0_scales[i] = to_columns.tile([P, CHUNK], U8, tag="f0_scales", name="f0_scales", align_bytes=64)
                codes, scales = f0_codes[i][:], f0_scales[i][:]
            nc.vector.quantize_mx(
                out=codes.bitcast(FP8X4), scales=scales, in_=f_grouped[i][:].rearrange("p a r t -> p (a r t)")
            )

        sim, conf0, sim_in, bar, conf1_t, larger = {}, {}, {}, {}, {}, {}
        row_max, row_sum, recip0, shift0, recip1, goal1, goal0 = {}, {}, {}, {}, {}, {}, {}
        sim_t_early, col_max_chunks, col_max, shift1, col_sum = {}, {}, {}, {}, {}
        recip1_diag, goal1_rep, goal1_bank, goal1_all = {}, {}, {}, {}
        inv_temp = 1.0 / TEMPERATURE

        def out_chunk(k, i):
            n, c = batch_and_bank(i)
            return out[k, n].rearrange("(p j) s -> p j s", j=per_part)[:, c * TILES : (c + 1) * TILES, :]

        def rows_matmul(i):
            n = batch_and_bank(i)[0]
            n_cols = slice(n * P, (n + 1) * P)
            sim[i] = psum_match.tile([P, TILES, P], F32, tag="sim", name="sim")
            for a in range(TILES):
                a_cols = slice(a * P, (a + 1) * P)
                nc.tensor.matmul_mx(
                    out=sim[i][:, a, :],
                    lhsT=f0_codes[i][:, a_cols].bitcast(FP8X4),
                    lhsT_scale=f0_scales[i][:, a_cols],
                    rhs=f1_codes[:, n_cols].bitcast(FP8X4),
                    rhs_scale=f1_scales[:, n_cols],
                    start=True,
                    stop=True,
                )

        def row_maxima(i):
            n, c = batch_and_bank(i)
            if c == 0:
                row_max[n] = by_batch.tile([P, per_part], F32, tag="row_max", name="row_max")
                recip0[n] = by_batch.tile([P, per_part], F32, tag="recip0", name="recip0")
                sim_in[n] = by_batch.tile(batch_shape, F32, tag="sim_in", name="sim_in")
            nc.vector.tensor_reduce(out=row_max[n][:, c * TILES : (c + 1) * TILES], in_=sim[i][:], axis=AXIS.X, op=ALU.max)

        def column_maxima_chunk(i):
            n, c = batch_and_bank(i)
            if c == 0:
                col_max_chunks[n] = by_batch.tile([P, banks], F32, tag="col_max_chunks", name="col_max_chunks")
            nc.vector.tensor_reduce(out=col_max_chunks[n][:, c : c + 1], in_=sim_t_early[i][:], axis=AXIS.X, op=ALU.max)

        def rows_shift(i):
            n, c = batch_and_bank(i)
            shift0[i] = late.tile([P, TILES], F32, tag="shift0", name="shift0")
            nc.scalar.mul(out=shift0[i][:], in_=row_max[n][:, c * TILES : (c + 1) * TILES], mul=-inv_temp)

        def rows_exp(i):
            n, c = batch_and_bank(i)
            row_sum[i] = late.tile([P, TILES], F32, tag="row_sum", name="row_sum")
            conf0[i] = to_mconf.tile([P, TILES, P], F32, tag="conf0", name="conf0")
            for a in range(TILES):
                nc.scalar.activation(
                    out=conf0[i][:, a, :],
                    in_=sim[i][:, a, :],
                    func=ACT.Exp,
                    bias=shift0[i][:, a : a + 1],
                    scale=inv_temp,
                    accum_out=row_sum[i][:, a : a + 1],
                )
            for a in range(0, TILES, 2):
                j = c * TILES + a
                nc.scalar.activation(
                    out=sim_in[n][:, j : j + 2],
                    in_=interior(sim[i][:])[:, a : a + 2],
                    func=ACT.Identity,
                    bias=sink[:, j : j + 1],
                    scale=1.0,
                )

        def column_maxima(n):
            col_max[n] = by_batch.tile([P, 1], F32, tag="col_max", name="col_max")
            nc.vector.tensor_reduce(out=col_max[n][:], in_=col_max_chunks[n][:], axis=AXIS.X, op=ALU.max)

        def column_shift(n):
            shift1[n] = by_batch.tile([P, 1], F32, tag="shift1", name="shift1")
            nc.scalar.mul(out=shift1[n][:], in_=col_max[n][:], mul=-inv_temp)
            col_sum[n] = by_batch.tile([P, banks], F32, tag="col_sum", name="col_sum")

        def finish_conf0(i):
            n, c = batch_and_bank(i)
            for a in range(TILES):
                j = c * TILES + a
                nc.scalar.activation(
                    out=conf0[i][:, a, :], in_=conf0[i][:, a, :], func=ACT.Copy, scale=recip0[n][:, j : j + 1]
                )
            nc.sync.dma_start(out=out_chunk(0, i), in_=conf0[i][:])

        def row_recips(i):
            n, c = batch_and_bank(i)
            nc.vector.reciprocal(out=recip0[n][:, c * TILES : (c + 1) * TILES], in_=row_sum[i][:])

        def columns_matmul(i, sim_t):
            n = batch_and_bank(i)[0]
            n_cols = slice(n * P, (n + 1) * P)
            nc.tensor.matmul_mx(
                out=sim_t[:],
                lhsT=f1_codes[:, n_cols].bitcast(FP8X4),
                lhsT_scale=f1_scales[:, n_cols],
                rhs=f0_codes[i][:].bitcast(FP8X4),
                rhs_scale=f0_scales[i][:],
                start=True,
                stop=True,
            )

        def columns_exp(i, sim_t):
            n, c = batch_and_bank(i)
            conf1_t[i] = to_back.tile([P, CHUNK], F32, tag="conf1_t", name="conf1_t")
            nc.scalar.activation(
                out=conf1_t[i][:],
                in_=sim_t[:],
                func=ACT.Exp,
                bias=shift1[n][:],
                scale=inv_temp,
                accum_out=col_sum[n][:, c : c + 1],
            )

        def sums_add(n):
            recip1[n] = late.tile([P, 1], F32, tag="recip1", name="recip1")
            nc.vector.tensor_reduce(out=recip1[n][:], in_=col_sum[n][:], axis=AXIS.X, op=ALU.add)

        def sums_recip(n):
            nc.vector.reciprocal(out=recip1[n][:], in_=recip1[n][:])

        def sums_diag(n):
            recip1_diag[n] = by_batch.tile([P, P], F32, tag="recip1_diag", name="recip1_diag")
            nc.vector.tensor_scalar_mul(out=recip1_diag[n][:], in0=ident[:], scalar1=recip1[n][:])

        def goal1_far(n):
            goal1[n] = late.tile([P, 1], F32, tag="goal1", name="goal1")
            nc.vector.tensor_scalar(
                out=goal1[n][:], in0=recip1[n][:], scalar1=THR, scalar2=FAR, op0=ALU.is_le, op1=ALU.mult
            )

        def goal1_add(n):
            nc.vector.tensor_tensor(out=goal1[n][:], in0=goal1[n][:], in1=col_max[n][:], op=ALU.add)

        def goal1_spread(n):
            goal1_rep[n] = late.tile([P, P], F32, tag="goal1_rep", name="goal1_rep")
            nc.vector.tensor_copy(out=goal1_rep[n][:], in_=goal1[n][:].to_broadcast([P, P]))

        def goal1_flip(n):
            goal1_bank[n] = psum_flip.tile([P, P], F32, tag="flipped", name="goal1_bank")
            nc.tensor.transpose(goal1_bank[n][:], goal1_rep[n][:], ident[:])

        def goal1_copy(n):
            goal1_all[n] = by_batch.tile([P, 1, P], F32, tag="goal1_all", name="goal1_all")
            nc.scalar.copy(out=goal1_all[n][:, 0, :], in_=goal1_bank[n][:])

        def back_matmul(i):
            n = batch_and_bank(i)[0]
            conf1_bank = psum_match.tile([P, TILES, P], F32, tag="columns", bufs=2)
            for a in range(TILES):
                nc.tensor.matmul(
                    out=conf1_bank[:, a, :],
                    lhsT=conf1_t[i][:, a * P : (a + 1) * P],
                    rhs=recip1_diag[n][:],
                    start=True,
                    stop=True,
                )
            return conf1_bank

        def back_copy(i, conf1_bank):
            conf1 = late.tile([P, TILES, P], F32, tag="conf1")
            nc.scalar.copy(out=conf1[:], in_=conf1_bank[:])
            nc.sync.dma_start(out=out_chunk(1, i), in_=conf1[:])

        def larger_chunk(i, conf1_bank):
            n, c = batch_and_bank(i)
            if c == 0:
                larger[n] = by_batch.tile(batch_shape, F32, tag="larger", name="larger")
            nc.vector.tensor_tensor(
                out=larger[n][:, c * TILES : (c + 1) * TILES],
                in0=interior(conf1_bank[:]),
                in1=interior(conf0[i][:]),
                op=ALU.max,
            )

        def goal0_far(n):
            goal0[n] = late.tile([P, per_part], F32, tag="goal0", name="goal0")
            nc.vector.tensor_scalar(
                out=goal0[n][:], in0=recip0[n][:], scalar1=THR, scalar2=FAR, op0=ALU.is_le, op1=ALU.mult
            )

        def goal0_add(n):
            nc.vector.tensor_tensor(out=goal0[n][:], in0=goal0[n][:], in1=row_max[n][:], op=ALU.add)

        def batch_bar(n):
            bar[n] = by_batch.tile(batch_shape, F32, tag="bar", name="bar")
            nc.vector.tensor_tensor(
                out=bar[n][:],
                in0=goal0[n][:].unsqueeze(2).unsqueeze(3).to_broadcast(batch_shape),
                in1=interior(goal1_all[n][:]).to_broadcast(batch_shape),
                op=ALU.min,
            )

        def batch_kept(n):
            nc.vector.tensor_tensor(out=bar[n][:], in0=sim_in[n][:], in1=bar[n][:], op=ALU.is_ge)

        def batch_mconf(n, first, last):
            mconf = mconf_tiles[n % len(mconf_tiles)]
            nc.vector.tensor_tensor(
                out=interior(mconf[:])[:, first:last], in0=bar[n][:, first:last], in1=larger[n][:, first:last], op=ALU.mult
            )
            nc.sync.dma_start(
                out=out[2, n].rearrange("(p j) s -> p j s", j=per_part)[:, first:last, :], in_=mconf[:, first:last, :]
            )

        w_rows = keep.tile([P, PACK * FEAT], BF16)
        nc.sync.dma_start(out=w_rows[:], in_=W.rearrange("(p t) k -> p (t k)", t=PACK))
        f1_rows = keep.tile([P, batches * FEAT], BF16)
        for i in range(batches // TILES):
            nc.sync.dma_start(
                out=f1_rows[:, i * TILES * FEAT : (i + 1) * TILES * FEAT].rearrange("s (n k) -> s n k", n=TILES),
                in_=feat_c1[i * TILES : (i + 1) * TILES].rearrange("n s k -> s n k"),
            )
        b_raw = keep.tile([P, PACK], BF16)
        nc.sync.dma_start(out=b_raw[:], in_=b.rearrange("(p t) -> p t", t=PACK))
        load_batch(0)
        load_batch(1)

        w_codes = keep.tile([P, FEAT], U32, align_bytes=64)
        w_scales = keep.tile([P, FEAT], U8, align_bytes=64)
        f1_codes = keep.tile([P, batches * P], U32, align_bytes=64)
        f1_scales = keep.tile([P, batches * P], U8, align_bytes=64)

        inv_scale = 1.0 / float(FEAT) ** 0.5
        bias = keep.tile([P, PACK], F32)
        nc.vector.tensor_single_scalar(out=bias[:], in_=b_raw[:], scalar=inv_scale, op=ALU.mult)
        bias_by_row = bias[:].unsqueeze(1).to_broadcast([P, P, PACK])

        w_grouped = flip_rows(w_rows[:], psum_proj, "acc")
        flip(0)
        nc.vector.quantize_mx(out=w_codes[:].bitcast(FP8X4), scales=w_scales[:], in_=w_grouped[:])
        quantise_x(0, pieces=2)
        flip(1)
        for g in range(LEAD):
            project_tile(g)

        def last_of_batch(i):
            if is_f0_chunk(i) and batch_and_bank(i)[1] == banks - 1:
                return batch_and_bank(i)[0]
            return None

        for i in range(n_chunks + MCONF):
            n, c = divmod(i, banks)
            if c == 0 and n + 2 < batches:
                load_batch(n + 2)
            maxima_due = last_of_batch(i - ROWS - 1)
            sums_due = last_of_batch(i - COLUMNS - 1)
            bar_due = last_of_batch(i - BAR)
            kept_due = last_of_batch(i - KEPT)
            mconf_due = last_of_batch(i - MCONF)
            for slot in range(TILES):
                g = i * TILES + slot
                if by_scalar(i):
                    if slot == 0:
                        project_tile(g + LEAD)
                        project_tile(g + LEAD + 1)
                    if slot < 2:
                        empty_tile(i * TILES + 2 * slot)
                        empty_tile(i * TILES + 2 * slot + 1)
                    if slot >= 2 and is_chunk(i + 1):
                        project_tile(g + LEAD)
                    if slot == 3:
                        interleave_f(i)
                else:
                    if is_chunk((g + LEAD) // TILES):
                        project_tile(g + LEAD)
                    if is_chunk(i - PROJECT):
                        empty_tile(g)
                if slot == 0:
                    if is_chunk(i - ROWS):
                        quantise_f(i - ROWS)
                    if sums_due is not None:
                        sums_add(sums_due)
                    if is_chunk(i - QUANTISE_X):
                        quantise_x(i - QUANTISE_X)
                    if sums_due is not None:
                        sums_recip(sums_due)
                    if is_chunk(i - FLIP):
                        flip(i - FLIP)
                    if bar_due is not None:
                        goal0_far(bar_due)
                if slot == 1:
                    if is_f0_chunk(i - ROWS):
                        rows_matmul(i - ROWS)
                        sim_t_early[i - ROWS] = psum_match.tile([P, CHUNK], F32, tag="columns", name="sim_t_early", bufs=2)
                        columns_matmul(i - ROWS, sim_t_early[i - ROWS])
                    if maxima_due is not None:
                        column_shift(maxima_due)
                    if is_f0_chunk(i - COLUMNS):
                        sim_t = psum_flip.tile([P, CHUNK], F32, tag="flipped")
                        columns_matmul(i - COLUMNS, sim_t)
                    if is_f0_chunk(i - FINISH_ROWS):
                        row_recips(i - FINISH_ROWS)
                    if sums_due is not None:
                        sums_diag(sums_due)
                        goal1_far(sums_due)
                    if bar_due is not None:
                        goal0_add(bar_due)
                    if kept_due is not None:
                        batch_kept(kept_due)
                    if sums_due is not None:
                        goal1_add(sums_due)
                    if mconf_due is not None:
                        batch_mconf(mconf_due, 0, per_part - TILES)
                if slot == 2:
                    if is_f0_chunk(i - ROWS):
                        row_maxima(i - ROWS)
                    if sums_due is not None:
                        goal1_spread(sums_due)
                    if is_f0_chunk(i - FINISH_ROWS):
                        finish_conf0(i - FINISH_ROWS)
                    if is_f0_chunk(i - COLUMNS):
                        columns_exp(i - COLUMNS, sim_t)
                    if sums_due is not None:
                        goal1_flip(sums_due)
                    if is_f0_chunk(i - BACK):
                        conf1_bank = back_matmul(i - BACK)
                if slot == 3:
                    if is_f0_chunk(i - ROWS):
                        column_maxima_chunk(i - ROWS)
                        rows_shift(i - ROWS)
                    if is_f0_chunk(i - BACK):
                        back_copy(i - BACK, conf1_bank)
                        larger_chunk(i - BACK, conf1_bank)
                    if is_f0_chunk(i - ROWS):
                        rows_exp(i - ROWS)
                    if bar_due is not None:
                        batch_bar(bar_due)
                    if mconf_due is not None:
                        batch_mconf(mconf_due, per_part - TILES, per_part)
                    if last_of_batch(i - ROWS) is not None:
                        column_maxima(last_of_batch(i - ROWS))
                    if sums_due is not None:
                        goal1_copy(sums_due)
